import numpy as np
import ml_dtypes


def mxq(x, axis, fmt="e4m3"):
    dtype, down = {"e4m3": (ml_dtypes.float8_e4m3fn, 7), "e5m2": (ml_dtypes.float8_e5m2, 14)}[fmt]
    v = np.moveaxis(np.asarray(x, np.float32).astype(ml_dtypes.bfloat16).astype(np.float64), axis, -1)
    blocks = v.reshape(v.shape[:-1] + (-1, 32))
    amax = np.abs(blocks).max(-1, keepdims=True)
    byte = np.maximum(np.where(amax > 0, np.frexp(amax)[1] - 1 + 127, 0) - down, 1)
    scale = np.exp2(byte - 127.0)
    codes = (blocks / scale).astype(np.float32).astype(dtype).astype(np.float64)
    return np.moveaxis((codes * scale).reshape(v.shape), -1, axis)


WIDE = False


def mx_kscale(k):
    if not WIDE:
        return np.ones(k)
    levels = np.array([10, -10, 5, -5, 0])
    if k % 512:
        return np.exp2(np.random.permutation(np.resize(levels, k // 32))).repeat(32)
    a = np.empty((k // 512, 16))
    for p in range(k // 512):
        a[p, :8] = np.random.permutation(np.resize(levels, 8))
        for g in range(8):
            far = levels[np.abs(levels - a[p, g]) >= 10]
            a[p, g + 8] = far[np.random.randint(len(far))]
    return np.exp2(a.ravel()).repeat(32)


BF16 = ml_dtypes.bfloat16


def bf(x):
    return np.asarray(x, np.float32).astype(BF16)


def f64(x):
    return np.asarray(x).astype(np.float64)


B, S, Dm, H = 2, 128, 2048, 16
D = Dm // H
ROPE_BASE = 10000.0


def _rope(t):
    theta = 1.0 / (ROPE_BASE ** (np.arange(0, D, 2, dtype=np.float64) / D))
    pos = np.arange(H, dtype=np.float64)[:, None]
    ang = pos * theta
    sin, cos = np.sin(ang), np.cos(ang)
    te, to = t[..., 0::2], t[..., 1::2]
    re = te * cos - to * sin
    ro = te * sin + to * cos
    return np.stack([re, ro], axis=-1).reshape(B, S, H, D)


def draw0():
    s = mx_kscale(Dm)
    sc = 1.0 / np.sqrt(Dm)
    return {"x": bf(np.random.standard_normal((B, S, Dm)) * s),
            "Wq": bf(np.random.standard_normal((Dm, Dm)) * sc / s[:, None]),
            "Wk": bf(np.random.standard_normal((Dm, Dm)) * sc / s[:, None]),
            "Wv": bf(np.random.standard_normal((Dm, Dm)) * sc / s[:, None]),
            "st_pos": 0}


def core(x, Wq, Wk, Wv, st_pos):
    xq = mxq(f64(x), 2, "e4m3")
    q = (xq @ mxq(f64(Wq), 0, "e4m3")).reshape(B, S, H, D)
    k = (xq @ mxq(f64(Wk), 0, "e4m3")).reshape(B, S, H, D)
    v = (xq @ mxq(f64(Wv), 0, "e4m3")).reshape(B, S, H, D)
    q = _rope(q)
    k = _rope(k)
    return q, k, v


def e4m3fn_bytes(y):
    return np.clip(np.asarray(y, np.float64), -448.0, 448.0).astype(np.float32).astype(ml_dtypes.float8_e4m3fn).view(np.uint8)


def e4m3fn_values(b):
    return np.asarray(b, np.uint8).view(ml_dtypes.float8_e4m3fn).astype(np.float64)


def setup_inputs():
    d = draw0()
    x0 = np.asarray(d['Wv']).astype(np.float64)
    s = (np.max(np.abs(x0), axis=(1,), keepdims=True) / 448.0).astype(np.float32)
    out = {}
    for k, v in d.items():
        if k == 'Wv':
            out['Wv_bytes'] = e4m3fn_bytes(x0 / s.astype(np.float64))
            out['Wv_scale'] = s
        else:
            out[k] = v
    return out


def reference(x, Wq, Wk, Wv_bytes, Wv_scale, st_pos):
    return core(x, Wq, Wk, e4m3fn_values(Wv_bytes) * Wv_scale.astype(np.float64), st_pos)

@@ -1,0 +1,395 @@
+from contextlib import ExitStack
+
+import concourse.mybir as mybir
+from concourse.masks import make_identity
+
+F32 = mybir.dt.float32
+BF16 = mybir.dt.bfloat16
+U32 = mybir.dt.uint32
+U8 = mybir.dt.uint8
+I32 = mybir.dt.int32
+FP8 = mybir.dt.float8_e4m3fn
+FP8X4 = mybir.dt.float8_e4m3fn_x4
+ALU = mybir.AluOpType
+ACT = mybir.ActivationFunctionType
+
+FLOPS = 2 * 256 * 2048 * 6144
+
+P = 128
+HEADS = 16
+ROPE_BASE = 10000.0
+PI = 3.141592653589793
+
+N_RAW = 6
+N_BYT = 4
+LEAD_WIDEN = 5
+LEAD_SINT = 3
+S_EVERY = 3
+N_CODV = 6
+OUT_WAIT = 1
+N_WIDE = 5
+N_GRP = 6
+N_OUT = 8
+S_ITEMS = (1, 3, 5, 7, 10, 13, 16, 19, 22, 25, 28, 31)
+S_DIAG = 10
+X_ENG = "S"
+D_MM = 1
+D_EVT = 2
+D_ROT = 1
+D_OUT = 5
+D_VOUT = 2
+V_ENG = ("S", "S")
+T_ENG = ("S", "S")
+O_ENG = ("S", "S")
+
+
+def build_order():
+    qk = []
+    for g in range(4):
+        qk.extend([("q", 0, g), ("q", 1, g)])
+    for mat, c in (("k", 0), ("k", 1), ("q", 2), ("q", 3), ("k", 2), ("k", 3)):
+        qk.extend([(mat, c, g) for g in range(4)])
+    vv = []
+    for half in range(2):
+        for g in range(4):
+            vv.extend([("v", 2 * half, g), ("v", 2 * half + 1, g)])
+    order = vv[:4]
+    rest = vv[4:]
+    for i, it in enumerate(qk):
+        order.append(it)
+        if i % 8 in (1, 4, 7) and len(rest) > 2:
+            order.append(rest[0])
+            rest = rest[1:]
+    order.extend(rest)
+    return order
+
+
+def tile_selfattention_kernel(tc, x, Wq, Wk, Wv_bytes, Wv_scale, st_pos, out_0, out_1, out_2):
+    nc = tc.nc
+    order = build_order()
+    n_items = len(order)
+    weights = {"q": Wq, "k": Wk}
+    outs = {"q": out_0, "k": out_1, "v": out_2}
+
+    with ExitStack() as ctx:
+        const = ctx.enter_context(tc.tile_pool(name="const", bufs=1))
+        raw = ctx.enter_context(tc.tile_pool(name="raw", bufs=N_RAW))
+        byt = ctx.enter_context(tc.tile_pool(name="byt", bufs=N_BYT))
+        wide = ctx.enter_context(tc.tile_pool(name="wide", bufs=N_WIDE))
+        grp = ctx.enter_context(tc.tile_pool(name="grp", bufs=N_GRP))
+        cod = ctx.enter_context(tc.tile_pool(name="cod", bufs=3))
+        codv = ctx.enter_context(tc.tile_pool(name="codv", bufs=N_CODV))
+        tsb = ctx.enter_context(tc.tile_pool(name="tsb", bufs=3))
+        outp = ctx.enter_context(tc.tile_pool(name="outp", bufs=N_OUT))
+        psum = ctx.enter_context(tc.psum_pool(name="psum", bufs=2))
+        ctx.enter_context(tc.manual_schedule())
+
+        def unit_of(it):
+            return (it[0], it[1] // 2, it[2])
+
+        need = {}
+        for n, it in enumerate(order):
+            u = unit_of(it)
+            key = n - (LEAD_WIDEN + 2 if it[0] == "v" else 0)
+            need[u] = min(need.get(u, key), key)
+        load_list = sorted(need, key=lambda u: need[u])
+        pending = {"v": [u for u in load_list if u[0] == "v"], "w": [u for u in load_list if u[0] != "v"]}
+        live = {"v": [], "w": []}
+        units = {}
+        reads_left = {}
+
+        def load(u):
+            mat, half, g = u
+            rows = slice(512 * g, 512 * (g + 1))
+            cols = slice(1024 * half, 1024 * (half + 1))
+            if mat == "v":
+                t = byt.tile([P, 4, 1024], U8, name="vb")
+                src = Wv_bytes
+            else:
+                t = raw.tile([P, 4, 1024], BF16, name="rw")
+                src = weights[mat]
+            nc.sync.dma_start(out=t[:], in_=src[rows, cols].rearrange("(p j) n -> p j n", j=4))
+            units[u] = t
+            reads_left[u] = 2
+            live["v" if mat == "v" else "w"].append(u)
+
+        def unit_read(u):
+            reads_left[u] = reads_left[u] - 1
+            kind = "v" if u[0] == "v" else "w"
+            while pending[kind] and live[kind] and reads_left[live[kind][0]] == 0:
+                live[kind].remove(live[kind][0])
+                nxt = pending[kind][0]
+                pending[kind].remove(nxt)
+                load(nxt)
+
+        vsc = const.tile([P, 4, 4], F32, name="vsc")
+        nc.sync.dma_start(out=vsc[:], in_=Wv_scale.rearrange("(g p j) o -> p g (j o)", p=P, j=4))
+        x_sb = const.tile([P, 2, 2048], BF16, name="x_sb")
+        first = []
+        nv, nw = 0, 0
+        for u in load_list:
+            if u[0] == "v" and nv < N_BYT:
+                first.append(u)
+                nv += 1
+            if u[0] != "v" and nw < N_RAW:
+                first.append(u)
+                nw += 1
+        for i, u in enumerate(first):
+            pending["v" if u[0] == "v" else "w"].remove(u)
+            load(u)
+            if i == 0:
+                nc.sync.dma_start(out=x_sb[:], in_=x.rearrange("b s d -> s b d"))
+
+        ident = const.tile([P, P], F32, name="ident")
+        make_identity(nc, ident[:])
+        pidx = const.tile([P, 1], I32, name="pidx")
+        nc.gpsimd.iota(pidx[:], pattern=[[0, 1]], base=0, channel_multiplier=1)
+        hidx = const.tile([P, HEADS], I32, name="hidx")
+        nc.gpsimd.iota(hidx[:], pattern=[[1, HEADS]], base=0, channel_multiplier=0)
+
+        zero = const.tile([P, 1], F32, name="zero")
+        nc.vector.memset(zero[:], 0.0)
+        warm = const.tile([P, 1], F32, name="warm")
+        nc.scalar.activation(out=warm[:], in_=zero[:], func=ACT.Sin)
+
+        bits = const.tile([P, 7], I32, name="bits")
+        for b in range(7):
+            nc.vector.tensor_scalar(out=bits[:, b : b + 1], in0=pidx[:], scalar1=b, scalar2=1,
+                                    op0=ALU.logical_shift_right, op1=ALU.bitwise_and)
+        fac = const.tile([P, 7], F32, name="fac")
+        nc.vector.tensor_scalar(out=fac[:, 0:1], in0=bits[:, 0:1], scalar1=-2.0, scalar2=1.0, op0=ALU.mult, op1=ALU.add)
+        for b in range(1, 7):
+            step = ROPE_BASE ** (-(2.0 ** (b - 1)) / 64.0)
+            nc.vector.tensor_scalar(out=fac[:, b : b + 1], in0=bits[:, b : b + 1], scalar1=step - 1.0, scalar2=1.0,
+                                    op0=ALU.mult, op1=ALU.add)
+        th3 = const.tile([P, 3], F32, name="th3")
+        nc.vector.tensor_tensor(out=th3[:], in0=fac[:, 1:4], in1=fac[:, 4:7], op=ALU.mult)
+        th1 = const.tile([P, 1], F32, name="th1")
+        nc.vector.tensor_tensor(out=th1[:], in0=th3[:, 0:1], in1=th3[:, 1:2], op=ALU.mult)
+        theta = const.tile([P, 1], F32, name="theta")
+        nc.vector.tensor_tensor(out=theta[:], in0=th1[:], in1=th3[:, 2:3], op=ALU.mult)
+        ang = const.tile([P, 2 * HEADS], F32, name="ang")
+        nc.vector.tensor_scalar(out=ang[:, 0:HEADS], in0=hidx[:], scalar1=theta[:, 0:1], scalar2=None, op0=ALU.mult)
+        nc.vector.tensor_scalar(out=ang[:, HEADS : 2 * HEADS], in0=hidx[:], scalar1=theta[:, 0:1], scalar2=PI / 2,
+                                op0=ALU.mult, op1=ALU.add)
+        turn1 = const.tile([P, 2 * HEADS], F32, name="turn1")
+        nc.vector.tensor_scalar(out=turn1[:], in0=ang[:], scalar1=PI, scalar2=None, op0=ALU.is_ge)
+        turn2 = const.tile([P, 2 * HEADS], F32, name="turn2")
+        nc.vector.scalar_tensor_tensor(out=turn2[:], in0=ang[:], scalar=3 * PI, in1=turn1[:], op0=ALU.is_ge, op1=ALU.add)
+        turn3 = const.tile([P, 2 * HEADS], F32, name="turn3")
+        nc.vector.scalar_tensor_tensor(out=turn3[:], in0=ang[:], scalar=5 * PI, in1=turn2[:], op0=ALU.is_ge, op1=ALU.add)
+        red = const.tile([P, 2 * HEADS], F32, name="red")
+        nc.vector.scalar_tensor_tensor(out=red[:], in0=turn3[:], scalar=-2 * PI, in1=ang[:], op0=ALU.mult, op1=ALU.add)
+        sc = const.tile([P, 2 * HEADS], F32, name="sc")
+        nc.scalar.activation(out=sc[:], in_=red[:], func=ACT.Sin)
+        ssin = const.tile([P, HEADS], F32, name="ssin")
+        nc.vector.tensor_scalar(out=ssin[:], in0=sc[:, 0:HEADS], scalar1=fac[:, 0:1], scalar2=None, op0=ALU.mult)
+        swp = const.tile([P, P], F32, name="swp")
+        swp_v = swp[:].rearrange("p (i e) -> p i e", e=2)
+        id_v = ident[:].rearrange("p (i e) -> p i e", e=2)
+        nc.vector.tensor_copy(out=swp_v[:, :, 0:1], in_=id_v[:, :, 1:2])
+        nc.vector.tensor_copy(out=swp_v[:, :, 1:2], in_=id_v[:, :, 0:1])
+        diag = const.tile([P, HEADS, P], F32, name="diag")
+        rmat = const.tile([P, HEADS, P], F32, name="rmat")
+        for h in range(HEADS):
+            if h < S_DIAG:
+                nc.scalar.activation(out=diag[:, h, :], in_=ident[:], func=ACT.Copy, scale=sc[:, HEADS + h : HEADS + h + 1])
+            else:
+                nc.vector.tensor_scalar(out=diag[:, h, :], in0=ident[:], scalar1=sc[:, HEADS + h : HEADS + h + 1], scalar2=None,
+                                        op0=ALU.mult)
+        for h in range(HEADS):
+            nc.vector.scalar_tensor_tensor(out=rmat[:, h, :], in0=swp[:], scalar=ssin[:, h : h + 1], in1=diag[:, h, :],
+                                           op0=ALU.mult, op1=ALU.add)
+
+        xq = const.tile([P, 4, 256], U32, name="xq", align_bytes=64)
+        xs = const.tile([P, 4, 256], U8, name="xs", align_bytes=64)
+        words = x_sb[:].rearrange("p b d -> p (b d)").bitcast(F32)
+        xg_tiles = []
+
+        def evac(eng, dst, src):
+            if eng == "S":
+                nc.scalar.copy(out=dst, in_=src)
+            else:
+                nc.vector.tensor_copy(out=dst, in_=src)
+
+        def x_transpose(g):
+            xt = psum.tile([P, 512], F32, name="acc", bufs=4)
+            for t in range(2):
+                for u in range(2):
+                    lo = 1024 * t + 256 * g + u
+                    nc.tensor.transpose(xt[:, 128 * (2 * t + u) : 128 * (2 * t + u + 1)], words[:, lo : lo + 255 : 2], ident[:])
+            xg = grp.tile([P, 1024], BF16, name="xg", bufs=4, align_bytes=64)
+            evac(X_ENG, xg[:].bitcast(F32).rearrange("p (t r u) -> p t r u", t=2, u=2),
+                 xt[:].rearrange("p (t u r) -> p t r u", t=2, u=2))
+            xg_tiles.append(xg)
+
+        def x_quant(g):
+            nc.vector.quantize_mx(out=xq[:, g, :].bitcast(FP8X4), scales=xs[:, g, :], in_=xg_tiles[g][:])
+
+        wd_tiles = {}
+        gr_tiles = {}
+        code = {}
+        acc = {}
+        tasks = {}
+        done = {}
+        qk_count = [0]
+        s_inter = {}
+        for n, it in enumerate(order):
+            if it[0] != "v":
+                s_inter[n] = qk_count[0] in S_ITEMS
+                qk_count[0] += 1
+            else:
+                s_inter[n] = False
+
+        def later(step, fn):
+            tasks.setdefault(step, []).append(fn)
+
+        def widen(n):
+            mat, c, g = order[n]
+            u = unit_of(order[n])
+            wd = wide.tile([P, 4, 512], BF16, name="wd")
+            lo = 512 * (c % 2)
+            for j in range(4):
+                nc.scalar.activation(out=wd[:, j, :], in_=units[u][:, j, lo : lo + 512].bitcast(FP8), func=ACT.Copy,
+                                     scale=vsc[:, g, j : j + 1])
+            wd_tiles[n] = wd
+            unit_read(u)
+
+        def inter(n):
+            mat, c, g = order[n]
+            gr = grp.tile([P, 2048], BF16, name="gr", align_bytes=64)
+            if mat == "v":
+                src = wd_tiles[n][:]
+            else:
+                lo = 512 * (c % 2)
+                src = units[unit_of(order[n])][:, :, lo : lo + 512]
+            dst = gr[:].rearrange("p (n j) -> p n j", j=4)
+            if s_inter[n]:
+                nc.scalar.copy(out=dst, in_=src.rearrange("p j n -> p n j"))
+            else:
+                nc.vector.tensor_copy(out=dst, in_=src.rearrange("p j n -> p n j"))
+            gr_tiles[n] = gr
+            if mat != "v":
+                unit_read(unit_of(order[n]))
+
+        def store(mat, t, c, tile_):
+            nc.sync.dma_start(out=outs[mat][t].rearrange("s h d -> s (h d)")[:, 512 * c : 512 * (c + 1)], in_=tile_[:])
+
+        def v_matmul(n, cv, sv):
+            mat, c, g = order[n]
+            for t in range(2):
+                if g == 0:
+                    acc[(c, t)] = psum.tile([P, 512], F32, name="acc", bufs=4)
+                nc.tensor.matmul_mx(out=acc[(c, t)][:], lhsT=xq[:, g, 128 * t : 128 * (t + 1)].bitcast(FP8X4),
+                                    lhsT_scale=xs[:, g, 128 * t : 128 * (t + 1)], rhs=cv[:].bitcast(FP8X4), rhs_scale=sv[:],
+                                    start=(g == 0), stop=(g == 3))
+
+        def v_out(c, engs):
+            for t in range(2):
+                ot = outp.tile([P, 512], F32, name="ot")
+                evac(engs[t], ot[:], acc[(c, t)][:])
+                store("v", t, c, ot)
+
+        def qk_matmul(mat, c, pair, hold):
+            cq, sq = code[(mat, c)]
+            tt = psum.tile([P, 512], F32, name="tT", bufs=2)
+            for hl in range(2):
+                hh = 2 * pair + hl
+                for g in range(4):
+                    nc.tensor.matmul_mx(out=tt[:, 256 * hl : 256 * (hl + 1)], lhsT=cq[:, g, 128 * hh : 128 * (hh + 1)].bitcast(FP8X4),
+                                        lhsT_scale=sq[:, g, 128 * hh : 128 * (hh + 1)], rhs=xq[:, g, :].bitcast(FP8X4),
+                                        rhs_scale=xs[:, g, :], start=(g == 0), stop=(g == 3))
+            hold[("tt", pair)] = tt
+
+        def qk_evac_t(pair, hold, eng):
+            ts = tsb.tile([P, 512], F32, name="ts")
+            evac(eng, ts[:], hold[("tt", pair)][:])
+            hold[("ts", pair)] = ts
+
+        def qk_rot(c, pair, hold):
+            if pair == 0:
+                for t in range(2):
+                    hold[("rot", t)] = psum.tile([P, 512], F32, name="rot", bufs=2)
+            for hl in range(2):
+                hh = 2 * pair + hl
+                for t in range(2):
+                    nc.tensor.matmul(out=hold[("rot", t)][:, 128 * hh : 128 * (hh + 1)],
+                                     lhsT=hold[("ts", pair)][:, 256 * hl + 128 * t : 256 * hl + 128 * (t + 1)],
+                                     rhs=rmat[:, 4 * c + hh, :], start=True, stop=True)
+
+        def qk_out(mat, c, hold, engs):
+            for t in range(2):
+                ot = outp.tile([P, 512], F32, name="ot")
+                evac(engs[t], ot[:], hold[("rot", t)][:])
+                store(mat, t, c, ot)
+
+        def quant(n, step):
+            mat, c, g = order[n]
+            if mat == "v":
+                cv = codv.tile([P, 512], U32, name="cv", align_bytes=64)
+                sv = codv.tile([P, 512], U8, name="sv", align_bytes=64)
+                nc.vector.quantize_mx(out=cv[:].bitcast(FP8X4), scales=sv[:], in_=gr_tiles[n][:])
+                later(step + 1, lambda: v_matmul(n, cv, sv))
+                if g == 3:
+                    later(step + D_VOUT, lambda: v_out(c, V_ENG))
+                return
+            if (mat, c) not in code:
+                cq_new = cod.tile([P, 4, 512], U32, name="cq", align_bytes=64)
+                sq_new = cod.tile([P, 4, 512], U8, name="sq", align_bytes=64)
+                code[(mat, c)] = (cq_new, sq_new)
+                done[(mat, c)] = 0
+            cq, sq = code[(mat, c)]
+            nc.vector.quantize_mx(out=cq[:, g, :].bitcast(FP8X4), scales=sq[:, g, :], in_=gr_tiles[n][:])
+            done[(mat, c)] = done[(mat, c)] + 1
+            if done[(mat, c)] == 4:
+                hold = {}
+                pair_queue.append((mat, c, 0, hold))
+                pair_queue.append((mat, c, 1, hold))
+
+        pair_queue = []
+        in_psum = []
+        to_store = []
+        tick = [0]
+
+        def epilogue_tick():
+            if to_store and (to_store[0][3] + OUT_WAIT <= tick[0] or (in_psum and in_psum[0][2] == 0)):
+                mat, c, hold, born = to_store[0]
+                to_store.remove(to_store[0])
+                qk_out(mat, c, hold, O_ENG)
+            tick[0] += 1
+            nxt = None
+            if pair_queue:
+                nxt = pair_queue[0]
+                pair_queue.remove(nxt)
+                qk_matmul(nxt[0], nxt[1], nxt[2], nxt[3])
+            if in_psum:
+                mat, c, pair, hold = in_psum[0]
+                in_psum.remove(in_psum[0])
+                qk_evac_t(pair, hold, T_ENG[pair])
+                qk_rot(c, pair, hold)
+                if pair == 1:
+                    to_store.append((mat, c, hold, tick[0]))
+            if nxt is not None:
+                in_psum.append(nxt)
+
+        for step in range(-LEAD_WIDEN - 1, n_items + 8):
+            for fn in tasks.get(step, []):
+                fn()
+            epilogue_tick()
+            n = step + LEAD_WIDEN
+            if 0 <= n < n_items and order[n][0] == "v":
+                widen(n)
+            n = step + LEAD_SINT
+            if 0 <= n < n_items and s_inter[n]:
+                inter(n)
+            n = step + 1
+            if 0 <= n < n_items and not s_inter[n]:
+                inter(n)
+            if step == -1:
+                for g in range(4):
+                    x_transpose(g)
+            if 0 <= step < n_items:
+                quant(step, step)
+            if step == 0:
+                for g in range(4):
+                    x_quant(g)

@@ -20,47 +20,37 @@ HEADS = 16
 ROPE_BASE = 10000.0
 PI = 3.141592653589793
 
-N_RAW = 6
+N_RAW = 8
 N_BYT = 4
-LEAD_WIDEN = 5
-LEAD_SINT = 3
-S_EVERY = 3
-N_CODV = 6
-OUT_WAIT = 1
 N_WIDE = 5
 N_GRP = 6
+N_COD = 3
+N_CODV = 6
+N_TSB = 4
 N_OUT = 8
-S_ITEMS = (1, 3, 5, 7, 10, 13, 16, 19, 22, 25, 28, 31)
+LEAD_WIDEN = 5
+LOAD_LEAD = 10
+LEAD_SINT = 3
+LAG_T = 2
+LAG_O = 3
+LAG_V = 2
 S_DIAG = 10
-X_ENG = "S"
-D_MM = 1
-D_EVT = 2
-D_ROT = 1
-D_OUT = 5
-D_VOUT = 2
-V_ENG = ("S", "S")
-T_ENG = ("S", "S")
-O_ENG = ("S", "S")
+X_ENG = "V"
+S_PLAN = ((1, 3), (1,), (1, 3), (1,), (1, 3), (1,), (1,), ())
+FAST_COPY = False
+TAIL_V = 3
 
 
 def build_order():
-    qk = []
-    for g in range(4):
-        qk.extend([("q", 0, g), ("q", 1, g)])
-    for mat, c in (("k", 0), ("k", 1), ("q", 2), ("q", 3), ("k", 2), ("k", 3)):
-        qk.extend([(mat, c, g) for g in range(4)])
-    vv = []
-    for half in range(2):
-        for g in range(4):
-            vv.extend([("v", 2 * half, g), ("v", 2 * half + 1, g)])
-    order = vv[:4]
-    rest = vv[4:]
-    for i, it in enumerate(qk):
-        order.append(it)
-        if i % 8 in (1, 4, 7) and len(rest) > 2:
-            order.append(rest[0])
-            rest = rest[1:]
-    order.extend(rest)
+    order = [("v", c, g) for c in (0, 1) for g in range(4)]
+    late_v = [("v", c, g) for c in (2, 3) for g in range(4)]
+    groups = (("q", 0), ("q", 1), ("k", 0), ("k", 1), ("q", 2), ("q", 3), ("k", 2), ("k", 3))
+    for i, (mat, c) in enumerate(groups):
+        order.extend([(mat, c, g) for g in range(4)])
+        if len(late_v) > TAIL_V or i == len(groups) - 1:
+            take = 1 if i < len(groups) - 1 else len(late_v)
+            order.extend(late_v[:take])
+            late_v = late_v[take:]
     return order
 
 
@@ -77,11 +67,11 @@ def tile_selfattention_kernel(tc, x, Wq, Wk, Wv_bytes, Wv_scale, st_pos, out_0, 
         byt = ctx.enter_context(tc.tile_pool(name="byt", bufs=N_BYT))
         wide = ctx.enter_context(tc.tile_pool(name="wide", bufs=N_WIDE))
         grp = ctx.enter_context(tc.tile_pool(name="grp", bufs=N_GRP))
-        cod = ctx.enter_context(tc.tile_pool(name="cod", bufs=3))
+        cod = ctx.enter_context(tc.tile_pool(name="cod", bufs=N_COD))
         codv = ctx.enter_context(tc.tile_pool(name="codv", bufs=N_CODV))
-        tsb = ctx.enter_context(tc.tile_pool(name="tsb", bufs=3))
+        tsb = ctx.enter_context(tc.tile_pool(name="tsb", bufs=N_TSB))
         outp = ctx.enter_context(tc.tile_pool(name="outp", bufs=N_OUT))
-        psum = ctx.enter_context(tc.psum_pool(name="psum", bufs=2))
+        psum = ctx.enter_context(tc.psum_pool(name="psum", bufs=3))
         ctx.enter_context(tc.manual_schedule())
 
         def unit_of(it):
@@ -89,10 +79,10 @@ def tile_selfattention_kernel(tc, x, Wq, Wk, Wv_bytes, Wv_scale, st_pos, out_0, 
 
         need = {}
         for n, it in enumerate(order):
-            u = unit_of(it)
-            key = n - (LEAD_WIDEN + 2 if it[0] == "v" else 0)
-            need[u] = min(need.get(u, key), key)
+            if unit_of(it) not in need:
+                need[unit_of(it)] = n - (LEAD_WIDEN if it[0] == "v" else LEAD_SINT)
         load_list = sorted(need, key=lambda u: need[u])
+        room = {"v": N_BYT, "w": N_RAW}
         pending = {"v": [u for u in load_list if u[0] == "v"], "w": [u for u in load_list if u[0] != "v"]}
         live = {"v": [], "w": []}
         units = {}
@@ -113,32 +103,30 @@ def tile_selfattention_kernel(tc, x, Wq, Wk, Wv_bytes, Wv_scale, st_pos, out_0, 
             reads_left[u] = 2
             live["v" if mat == "v" else "w"].append(u)
 
+        def load_next(kind):
+            nxt = pending[kind][0]
+            pending[kind].remove(nxt)
+            load(nxt)
+
         def unit_read(u):
             reads_left[u] = reads_left[u] - 1
-            kind = "v" if u[0] == "v" else "w"
-            while pending[kind] and live[kind] and reads_left[live[kind][0]] == 0:
-                live[kind].remove(live[kind][0])
-                nxt = pending[kind][0]
-                pending[kind].remove(nxt)
-                load(nxt)
+
+        def issue_loads(step):
+            for u in load_list:
+                kind = "v" if u[0] == "v" else "w"
+                if u in pending[kind] and need[u] - LOAD_LEAD <= step and pending[kind][0] == u:
+                    if len(live[kind]) == room[kind]:
+                        if reads_left[live[kind][0]] > 0:
+                            continue
+                        live[kind].remove(live[kind][0])
+                    load_next(kind)
 
         vsc = const.tile([P, 4, 4], F32, name="vsc")
         nc.sync.dma_start(out=vsc[:], in_=Wv_scale.rearrange("(g p j) o -> p g (j o)", p=P, j=4))
         x_sb = const.tile([P, 2, 2048], BF16, name="x_sb")
-        first = []
-        nv, nw = 0, 0
-        for u in load_list:
-            if u[0] == "v" and nv < N_BYT:
-                first.append(u)
-                nv += 1
-            if u[0] != "v" and nw < N_RAW:
-                first.append(u)
-                nw += 1
-        for i, u in enumerate(first):
-            pending["v" if u[0] == "v" else "w"].remove(u)
-            load(u)
-            if i == 0:
-                nc.sync.dma_start(out=x_sb[:], in_=x.rearrange("b s d -> s b d"))
+        load_next("v")
+        load_next("v")
+        nc.sync.dma_start(out=x_sb[:], in_=x.rearrange("b s d -> s b d"))
 
         ident = const.tile([P, P], F32, name="ident")
         make_identity(nc, ident[:])
@@ -159,8 +147,8 @@ def tile_selfattention_kernel(tc, x, Wq, Wk, Wv_bytes, Wv_scale, st_pos, out_0, 
         fac = const.tile([P, 7], F32, name="fac")
         nc.vector.tensor_scalar(out=fac[:, 0:1], in0=bits[:, 0:1], scalar1=-2.0, scalar2=1.0, op0=ALU.mult, op1=ALU.add)
         for b in range(1, 7):
-            step = ROPE_BASE ** (-(2.0 ** (b - 1)) / 64.0)
-            nc.vector.tensor_scalar(out=fac[:, b : b + 1], in0=bits[:, b : b + 1], scalar1=step - 1.0, scalar2=1.0,
+            ratio = ROPE_BASE ** (-(2.0 ** (b - 1)) / 64.0)
+            nc.vector.tensor_scalar(out=fac[:, b : b + 1], in0=bits[:, b : b + 1], scalar1=ratio - 1.0, scalar2=1.0,
                                     op0=ALU.mult, op1=ALU.add)
         th3 = const.tile([P, 3], F32, name="th3")
         nc.vector.tensor_tensor(out=th3[:], in0=fac[:, 1:4], in1=fac[:, 4:7], op=ALU.mult)
@@ -201,19 +189,19 @@ def tile_selfattention_kernel(tc, x, Wq, Wk, Wv_bytes, Wv_scale, st_pos, out_0, 
             nc.vector.scalar_tensor_tensor(out=rmat[:, h, :], in0=swp[:], scalar=ssin[:, h : h + 1], in1=diag[:, h, :],
                                            op0=ALU.mult, op1=ALU.add)
 
-        xq = const.tile([P, 4, 256], U32, name="xq", align_bytes=64)
-        xs = const.tile([P, 4, 256], U8, name="xs", align_bytes=64)
-        words = x_sb[:].rearrange("p b d -> p (b d)").bitcast(F32)
-        xg_tiles = []
-
         def evac(eng, dst, src):
             if eng == "S":
                 nc.scalar.copy(out=dst, in_=src)
             else:
                 nc.vector.tensor_copy(out=dst, in_=src)
 
+        xq = const.tile([P, 4, 256], U32, name="xq", align_bytes=64)
+        xs = const.tile([P, 4, 256], U8, name="xs", align_bytes=64)
+        words = x_sb[:].rearrange("p b d -> p (b d)").bitcast(F32)
+        xg_tiles = []
+
         def x_transpose(g):
-            xt = psum.tile([P, 512], F32, name="acc", bufs=4)
+            xt = psum.tile([P, 512], F32, name=("tT" if g < 3 else "rot"))
             for t in range(2):
                 for u in range(2):
                     lo = 1024 * t + 256 * g + u
@@ -231,15 +219,12 @@ def tile_selfattention_kernel(tc, x, Wq, Wk, Wv_bytes, Wv_scale, st_pos, out_0, 
         code = {}
         acc = {}
         tasks = {}
-        done = {}
-        qk_count = [0]
         s_inter = {}
+        group_no = {}
         for n, it in enumerate(order):
-            if it[0] != "v":
-                s_inter[n] = qk_count[0] in S_ITEMS
-                qk_count[0] += 1
-            else:
-                s_inter[n] = False
+            if it[0] != "v" and (it[0], it[1]) not in group_no:
+                group_no[(it[0], it[1])] = len(group_no)
+            s_inter[n] = it[0] != "v" and it[2] in S_PLAN[group_no[(it[0], it[1])]]
 
         def later(step, fn):
             tasks.setdefault(step, []).append(fn)
@@ -263,65 +248,83 @@ def tile_selfattention_kernel(tc, x, Wq, Wk, Wv_bytes, Wv_scale, st_pos, out_0, 
             else:
                 lo = 512 * (c % 2)
                 src = units[unit_of(order[n])][:, :, lo : lo + 512]
-            dst = gr[:].rearrange("p (n j) -> p n j", j=4)
-            if s_inter[n]:
-                nc.scalar.copy(out=dst, in_=src.rearrange("p j n -> p n j"))
+            if FAST_COPY:
+                dst = gr[:].rearrange("p (c i j) -> p c j i", i=4, j=4)
+                src = src.rearrange("p j (c i) -> p c j i", i=4)
             else:
-                nc.vector.tensor_copy(out=dst, in_=src.rearrange("p j n -> p n j"))
+                dst = gr[:].rearrange("p (n j) -> p n j", j=4)
+                src = src.rearrange("p j n -> p n j")
+            evac("S" if s_inter[n] else "V", dst, src)
             gr_tiles[n] = gr
             if mat != "v":
                 unit_read(unit_of(order[n]))
-
-        def store(mat, t, c, tile_):
-            nc.sync.dma_start(out=outs[mat][t].rearrange("s h d -> s (h d)")[:, 512 * c : 512 * (c + 1)], in_=tile_[:])
 
         def v_matmul(n, cv, sv):
             mat, c, g = order[n]
             for t in range(2):
                 if g == 0:
-                    acc[(c, t)] = psum.tile([P, 512], F32, name="acc", bufs=4)
-                nc.tensor.matmul_mx(out=acc[(c, t)][:], lhsT=xq[:, g, 128 * t : 128 * (t + 1)].bitcast(FP8X4),
+                    acc[t] = psum.tile([P, 512], F32, name="acc", bufs=2)
+                nc.tensor.matmul_mx(out=acc[t][:], lhsT=xq[:, g, 128 * t : 128 * (t + 1)].bitcast(FP8X4),
                                     lhsT_scale=xs[:, g, 128 * t : 128 * (t + 1)], rhs=cv[:].bitcast(FP8X4), rhs_scale=sv[:],
                                     start=(g == 0), stop=(g == 3))
 
         def v_out(c, engs):
             for t in range(2):
                 ot = outp.tile([P, 512], F32, name="ot")
-                evac(engs[t], ot[:], acc[(c, t)][:])
-                store("v", t, c, ot)
+                evac(engs[t], ot[:], acc[t][:])
+                nc.sync.dma_start(out=out_2[t].rearrange("s h d -> s (h d)")[:, 512 * c : 512 * (c + 1)], in_=ot[:])
 
-        def qk_matmul(mat, c, pair, hold):
+        head_queue = []
+        multiplied = []
+        rotated = []
+        slot = [0]
+
+        def head_matmul(hd):
+            mat, c, hh = hd["mat"], hd["c"], hd["hh"]
             cq, sq = code[(mat, c)]
-            tt = psum.tile([P, 512], F32, name="tT", bufs=2)
-            for hl in range(2):
-                hh = 2 * pair + hl
-                for g in range(4):
-                    nc.tensor.matmul_mx(out=tt[:, 256 * hl : 256 * (hl + 1)], lhsT=cq[:, g, 128 * hh : 128 * (hh + 1)].bitcast(FP8X4),
-                                        lhsT_scale=sq[:, g, 128 * hh : 128 * (hh + 1)], rhs=xq[:, g, :].bitcast(FP8X4),
-                                        rhs_scale=xs[:, g, :], start=(g == 0), stop=(g == 3))
-            hold[("tt", pair)] = tt
+            tt = psum.tile([P, 256], F32, name="tT")
+            for g in range(4):
+                nc.tensor.matmul_mx(out=tt[:], lhsT=cq[:, g, 128 * hh : 128 * (hh + 1)].bitcast(FP8X4),
+                                    lhsT_scale=sq[:, g, 128 * hh : 128 * (hh + 1)], rhs=xq[:, g, :].bitcast(FP8X4),
+                                    rhs_scale=xs[:, g, :], start=(g == 0), stop=(g == 3))
+            hd["tt"] = tt
 
-        def qk_evac_t(pair, hold, eng):
-            ts = tsb.tile([P, 512], F32, name="ts")
-            evac(eng, ts[:], hold[("tt", pair)][:])
-            hold[("ts", pair)] = ts
-
-        def qk_rot(c, pair, hold):
-            if pair == 0:
-                for t in range(2):
-                    hold[("rot", t)] = psum.tile([P, 512], F32, name="rot", bufs=2)
-            for hl in range(2):
-                hh = 2 * pair + hl
-                for t in range(2):
-                    nc.tensor.matmul(out=hold[("rot", t)][:, 128 * hh : 128 * (hh + 1)],
-                                     lhsT=hold[("ts", pair)][:, 256 * hl + 128 * t : 256 * hl + 128 * (t + 1)],
-                                     rhs=rmat[:, 4 * c + hh, :], start=True, stop=True)
-
-        def qk_out(mat, c, hold, engs):
+        def head_rotate(hd, pair_tile):
+            ts = tsb.tile([P, 256], F32, name="ts")
+            evac("S", ts[:], hd["tt"][:])
+            hl = hd["hh"] % 2
             for t in range(2):
-                ot = outp.tile([P, 512], F32, name="ot")
-                evac(engs[t], ot[:], hold[("rot", t)][:])
-                store(mat, t, c, ot)
+                nc.tensor.matmul(out=pair_tile[:, 256 * t + 128 * hl : 256 * t + 128 * (hl + 1)],
+                                 lhsT=ts[:, 128 * t : 128 * (t + 1)], rhs=rmat[:, 4 * hd["c"] + hd["hh"], :], start=True, stop=True)
+
+        def pair_out(hd, pair_tile, eng):
+            ot = outp.tile([P, 512], F32, name="ot")
+            evac(eng, ot[:], pair_tile[:])
+            lo = 512 * hd["c"] + 128 * (hd["hh"] - 1)
+            nc.sync.dma_start(out=outs[hd["mat"]].rearrange("b s h d -> s b (h d)")[:, :, lo : lo + 256],
+                              in_=ot[:].rearrange("p (t n) -> p t n", t=2))
+
+        pair_now = [None]
+
+        def epilogue_slot(drain):
+            slot[0] += 1
+            if rotated and (rotated[0][2] + LAG_O <= slot[0] or (drain and not head_queue and not multiplied)):
+                hd, pt, born = rotated[0]
+                rotated.remove(rotated[0])
+                pair_out(hd, pt, "S")
+            if head_queue:
+                hd = head_queue[0]
+                head_queue.remove(hd)
+                head_matmul(hd)
+                multiplied.append((hd, slot[0]))
+            if multiplied and (multiplied[0][1] + LAG_T <= slot[0] or (drain and not head_queue)):
+                hd = multiplied[0][0]
+                multiplied.remove(multiplied[0])
+                if hd["hh"] % 2 == 0:
+                    pair_now[0] = psum.tile([P, 512], F32, name="rot")
+                head_rotate(hd, pair_now[0])
+                if hd["hh"] % 2 == 1:
+                    rotated.append((hd, pair_now[0], slot[0]))
 
         def quant(n, step):
             mat, c, g = order[n]
@@ -331,51 +334,25 @@ def tile_selfattention_kernel(tc, x, Wq, Wk, Wv_bytes, Wv_scale, st_pos, out_0, 
                 nc.vector.quantize_mx(out=cv[:].bitcast(FP8X4), scales=sv[:], in_=gr_tiles[n][:])
                 later(step + 1, lambda: v_matmul(n, cv, sv))
                 if g == 3:
-                    later(step + D_VOUT, lambda: v_out(c, V_ENG))
+                    last = n == n_items - 1
+                    later(step + (1 if last else LAG_V), lambda: v_out(c, ("S", "V") if last else ("S", "S")))
                 return
-            if (mat, c) not in code:
+            if g == 0:
                 cq_new = cod.tile([P, 4, 512], U32, name="cq", align_bytes=64)
                 sq_new = cod.tile([P, 4, 512], U8, name="sq", align_bytes=64)
                 code[(mat, c)] = (cq_new, sq_new)
-                done[(mat, c)] = 0
             cq, sq = code[(mat, c)]
             nc.vector.quantize_mx(out=cq[:, g, :].bitcast(FP8X4), scales=sq[:, g, :], in_=gr_tiles[n][:])
-            done[(mat, c)] = done[(mat, c)] + 1
-            if done[(mat, c)] == 4:
-                hold = {}
-                pair_queue.append((mat, c, 0, hold))
-                pair_queue.append((mat, c, 1, hold))
+            if g == 3:
+                for hh in range(4):
+                    head_queue.append({"mat": mat, "c": c, "hh": hh})
 
-        pair_queue = []
-        in_psum = []
-        to_store = []
-        tick = [0]
-
-        def epilogue_tick():
-            if to_store and (to_store[0][3] + OUT_WAIT <= tick[0] or (in_psum and in_psum[0][2] == 0)):
-                mat, c, hold, born = to_store[0]
-                to_store.remove(to_store[0])
-                qk_out(mat, c, hold, O_ENG)
-            tick[0] += 1
-            nxt = None
-            if pair_queue:
-                nxt = pair_queue[0]
-                pair_queue.remove(nxt)
-                qk_matmul(nxt[0], nxt[1], nxt[2], nxt[3])
-            if in_psum:
-                mat, c, pair, hold = in_psum[0]
-                in_psum.remove(in_psum[0])
-                qk_evac_t(pair, hold, T_ENG[pair])
-                qk_rot(c, pair, hold)
-                if pair == 1:
-                    to_store.append((mat, c, hold, tick[0]))
-            if nxt is not None:
-                in_psum.append(nxt)
-
-        for step in range(-LEAD_WIDEN - 1, n_items + 8):
+        step = -LEAD_WIDEN - 1
+        while step < n_items + 2 or head_queue or multiplied or rotated:
+            issue_loads(step)
+            epilogue_slot(step >= n_items)
             for fn in tasks.get(step, []):
                 fn()
-            epilogue_tick()
             n = step + LEAD_WIDEN
             if 0 <= n < n_items and order[n][0] == "v":
                 widen(n)
@@ -393,3 +370,4 @@ def tile_selfattention_kernel(tc, x, Wq, Wk, Wv_bytes, Wv_scale, st_pos, out_0, 
             if step == 0:
                 for g in range(4):
                     x_quant(g)
+            step += 1

@@ -37,7 +37,7 @@ LAG_V = 2
 S_DIAG = 10
 X_ENG = "V"
 S_PLAN = ((1, 3), (1,), (1, 3), (1,), (1, 3), (1,), (1,), ())
-FAST_COPY = False
+FAST_COPY = True
 TAIL_V = 3
 
 

@@ -22,35 +22,38 @@ PI = 3.141592653589793
 
 N_RAW = 8
 N_BYT = 4
-N_WIDE = 5
-N_GRP = 6
+N_WIDE = 7
+N_GRP = 8
 N_COD = 3
-N_CODV = 6
-N_TSB = 4
+N_CODV = 8
+N_TSB = 6
 N_OUT = 8
 LEAD_WIDEN = 5
 LOAD_LEAD = 10
 LEAD_SINT = 3
 LAG_T = 2
 LAG_O = 3
+LAG_R = 1
 LAG_V = 2
 S_DIAG = 10
 X_ENG = "V"
 S_PLAN = ((1, 3), (1,), (1, 3), (1,), (1, 3), (1,), (1,), ())
 FAST_COPY = True
-TAIL_V = 3
+HEAD_V = 5
+V_AFTER = (1, 1, 1, 1, 1, 1, 1, 4)
+FAST_END = 8
 
 
 def build_order():
-    order = [("v", c, g) for c in (0, 1) for g in range(4)]
-    late_v = [("v", c, g) for c in (2, 3) for g in range(4)]
+    v_items = [("v", c, g) for c in range(4) for g in range(4)]
+    order = v_items[:HEAD_V]
+    v_items = v_items[HEAD_V:]
     groups = (("q", 0), ("q", 1), ("k", 0), ("k", 1), ("q", 2), ("q", 3), ("k", 2), ("k", 3))
     for i, (mat, c) in enumerate(groups):
         order.extend([(mat, c, g) for g in range(4)])
-        if len(late_v) > TAIL_V or i == len(groups) - 1:
-            take = 1 if i < len(groups) - 1 else len(late_v)
-            order.extend(late_v[:take])
-            late_v = late_v[take:]
+        order.extend(v_items[: V_AFTER[i]])
+        v_items = v_items[V_AFTER[i] :]
+    assert not v_items
     return order
 
 
@@ -96,7 +99,7 @@ def tile_selfattention_kernel(tc, x, Wq, Wk, Wv_bytes, Wv_scale, st_pos, out_0, 
                 t = byt.tile([P, 4, 1024], U8, name="vb")
                 src = Wv_bytes
             else:
-                t = raw.tile([P, 4, 1024], BF16, name="rw")
+                t = raw.tile([P, 4, 1024], BF16, name="rw", align_bytes=64)
                 src = weights[mat]
             nc.sync.dma_start(out=t[:], in_=src[rows, cols].rearrange("(p j) n -> p j n", j=4))
             units[u] = t
@@ -122,8 +125,12 @@ def tile_selfattention_kernel(tc, x, Wq, Wk, Wv_bytes, Wv_scale, st_pos, out_0, 
                     load_next(kind)
 
         vsc = const.tile([P, 4, 4], F32, name="vsc")
-        nc.sync.dma_start(out=vsc[:], in_=Wv_scale.rearrange("(g p j) o -> p g (j o)", p=P, j=4))
-        x_sb = const.tile([P, 2, 2048], BF16, name="x_sb")
+        nc.scalar.dma_start(out=vsc[:], in_=Wv_scale.rearrange("(g p j) o -> p g (j o)", p=P, j=4))
+        x_sb = raw.tile([P, 2, 2048], BF16, name="rw", align_bytes=64)
+        xg = raw.tile([P, 4, 1024], BF16, name="rw", align_bytes=64)
+        for u in (("x", 0, 0), ("x", 1, 0)):
+            live["w"].append(u)
+            reads_left[u] = 1
         load_next("v")
         load_next("v")
         nc.sync.dma_start(out=x_sb[:], in_=x.rearrange("b s d -> s b d"))
@@ -177,16 +184,15 @@ def tile_selfattention_kernel(tc, x, Wq, Wk, Wv_bytes, Wv_scale, st_pos, out_0, 
         id_v = ident[:].rearrange("p (i e) -> p i e", e=2)
         nc.vector.tensor_copy(out=swp_v[:, :, 0:1], in_=id_v[:, :, 1:2])
         nc.vector.tensor_copy(out=swp_v[:, :, 1:2], in_=id_v[:, :, 0:1])
-        diag = const.tile([P, HEADS, P], F32, name="diag")
         rmat = const.tile([P, HEADS, P], F32, name="rmat")
         for h in range(HEADS):
             if h < S_DIAG:
-                nc.scalar.activation(out=diag[:, h, :], in_=ident[:], func=ACT.Copy, scale=sc[:, HEADS + h : HEADS + h + 1])
+                nc.scalar.activation(out=rmat[:, h, :], in_=ident[:], func=ACT.Copy, scale=sc[:, HEADS + h : HEADS + h + 1])
             else:
-                nc.vector.tensor_scalar(out=diag[:, h, :], in0=ident[:], scalar1=sc[:, HEADS + h : HEADS + h + 1], scalar2=None,
+                nc.vector.tensor_scalar(out=rmat[:, h, :], in0=ident[:], scalar1=sc[:, HEADS + h : HEADS + h + 1], scalar2=None,
                                         op0=ALU.mult)
         for h in range(HEADS):
-            nc.vector.scalar_tensor_tensor(out=rmat[:, h, :], in0=swp[:], scalar=ssin[:, h : h + 1], in1=diag[:, h, :],
+            nc.vector.scalar_tensor_tensor(out=rmat[:, h, :], in0=swp[:], scalar=ssin[:, h : h + 1], in1=rmat[:, h, :],
                                            op0=ALU.mult, op1=ALU.add)
 
         def evac(eng, dst, src):
@@ -198,7 +204,6 @@ def tile_selfattention_kernel(tc, x, Wq, Wk, Wv_bytes, Wv_scale, st_pos, out_0, 
         xq = const.tile([P, 4, 256], U32, name="xq", align_bytes=64)
         xs = const.tile([P, 4, 256], U8, name="xs", align_bytes=64)
         words = x_sb[:].rearrange("p b d -> p (b d)").bitcast(F32)
-        xg_tiles = []
 
         def x_transpose(g):
             xt = psum.tile([P, 512], F32, name=("tT" if g < 3 else "rot"))
@@ -206,13 +211,12 @@ def tile_selfattention_kernel(tc, x, Wq, Wk, Wv_bytes, Wv_scale, st_pos, out_0, 
                 for u in range(2):
                     lo = 1024 * t + 256 * g + u
                     nc.tensor.transpose(xt[:, 128 * (2 * t + u) : 128 * (2 * t + u + 1)], words[:, lo : lo + 255 : 2], ident[:])
-            xg = grp.tile([P, 1024], BF16, name="xg", bufs=4, align_bytes=64)
-            evac(X_ENG, xg[:].bitcast(F32).rearrange("p (t r u) -> p t r u", t=2, u=2),
+            evac(X_ENG, xg[:, g, :].bitcast(F32).rearrange("p (t r u) -> p t r u", t=2, u=2),
                  xt[:].rearrange("p (t u r) -> p t r u", t=2, u=2))
-            xg_tiles.append(xg)
 
-        def x_quant(g):
-            nc.vector.quantize_mx(out=xq[:, g, :].bitcast(FP8X4), scales=xs[:, g, :], in_=xg_tiles[g][:])
+        def x_quant():
+            nc.vector.quantize_mx(out=xq[:].rearrange("p g n -> p (g n)").bitcast(FP8X4), scales=xs[:].rearrange("p g n -> p (g n)"),
+                                  in_=xg[:].rearrange("p g n -> p (g n)"))
 
         wd_tiles = {}
         gr_tiles = {}
@@ -276,6 +280,7 @@ def tile_selfattention_kernel(tc, x, Wq, Wk, Wv_bytes, Wv_scale, st_pos, out_0, 
 
         head_queue = []
         multiplied = []
+        emptied = []
         rotated = []
         slot = [0]
 
@@ -289,9 +294,13 @@ def tile_selfattention_kernel(tc, x, Wq, Wk, Wv_bytes, Wv_scale, st_pos, out_0, 
                                     rhs_scale=xs[:, g, :], start=(g == 0), stop=(g == 3))
             hd["tt"] = tt
 
-        def head_rotate(hd, pair_tile):
+        def head_evac(hd):
             ts = tsb.tile([P, 256], F32, name="ts")
             evac("S", ts[:], hd["tt"][:])
+            hd["ts"] = ts
+
+        def head_rotate(hd, pair_tile):
+            ts = hd["ts"]
             hl = hd["hh"] % 2
             for t in range(2):
                 nc.tensor.matmul(out=pair_tile[:, 256 * t + 128 * hl : 256 * t + 128 * (hl + 1)],
@@ -308,7 +317,7 @@ def tile_selfattention_kernel(tc, x, Wq, Wk, Wv_bytes, Wv_scale, st_pos, out_0, 
 
         def epilogue_slot(drain):
             slot[0] += 1
-            if rotated and (rotated[0][2] + LAG_O <= slot[0] or (drain and not head_queue and not multiplied)):
+            if rotated and (rotated[0][2] + LAG_O <= slot[0] or (drain and not head_queue and not multiplied and not emptied)):
                 hd, pt, born = rotated[0]
                 rotated.remove(rotated[0])
                 pair_out(hd, pt, "S")
@@ -320,6 +329,11 @@ def tile_selfattention_kernel(tc, x, Wq, Wk, Wv_bytes, Wv_scale, st_pos, out_0, 
             if multiplied and (multiplied[0][1] + LAG_T <= slot[0] or (drain and not head_queue)):
                 hd = multiplied[0][0]
                 multiplied.remove(multiplied[0])
+                head_evac(hd)
+                emptied.append((hd, slot[0]))
+            if emptied and (emptied[0][1] + LAG_R <= slot[0] or (drain and not head_queue and not multiplied)):
+                hd = emptied[0][0]
+                emptied.remove(emptied[0])
                 if hd["hh"] % 2 == 0:
                     pair_now[0] = psum.tile([P, 512], F32, name="rot")
                 head_rotate(hd, pair_now[0])
@@ -348,9 +362,10 @@ def tile_selfattention_kernel(tc, x, Wq, Wk, Wv_bytes, Wv_scale, st_pos, out_0, 
                     head_queue.append({"mat": mat, "c": c, "hh": hh})
 
         step = -LEAD_WIDEN - 1
-        while step < n_items + 2 or head_queue or multiplied or rotated:
+        while step < n_items + 2 or head_queue or multiplied or emptied or rotated:
             issue_loads(step)
-            epilogue_slot(step >= n_items)
+            for rep in range(2 if step >= n_items - FAST_END else 1):
+                epilogue_slot(step >= n_items)
             for fn in tasks.get(step, []):
                 fn()
             n = step + LEAD_WIDEN
@@ -365,9 +380,10 @@ def tile_selfattention_kernel(tc, x, Wq, Wk, Wv_bytes, Wv_scale, st_pos, out_0, 
             if step == -1:
                 for g in range(4):
                     x_transpose(g)
+                unit_read(("x", 0, 0))
             if 0 <= step < n_items:
                 quant(step, step)
             if step == 0:
-                for g in range(4):
-                    x_quant(g)
+                x_quant()
+                unit_read(("x", 1, 0))
             step += 1

@@ -21,11 +21,11 @@ ROPE_BASE = 10000.0
 PI = 3.141592653589793
 
 N_RAW = 8
-N_BYT = 4
+N_BYT = 6
 N_WIDE = 7
-N_GRP = 8
+N_GRP = 7
 N_COD = 3
-N_CODV = 8
+N_CODV = 6
 N_TSB = 6
 N_OUT = 8
 LEAD_WIDEN = 5
@@ -37,23 +37,29 @@ LAG_R = 1
 LAG_V = 2
 S_DIAG = 10
 X_ENG = "V"
-S_PLAN = ((1, 3), (1,), (1, 3), (1,), (1, 3), (1,), (1,), ())
+S_PLAN = ((1, 3), (1,), (1, 3), (1,), (1,), (1,), (1,), ())
 FAST_COPY = True
-HEAD_V = 5
-V_AFTER = (1, 1, 1, 1, 1, 1, 1, 4)
+PATTERN = "vvvvv" + "wwwwv" * 7 + "wwwwvvvv"
 FAST_END = 8
+NARROW = (("v", 0),)
+S_VITEMS = ()
+FIRST_LOADS = ("v", "v")
+X_STEP = -1
 
 
 def build_order():
     v_items = [("v", c, g) for c in range(4) for g in range(4)]
-    order = v_items[:HEAD_V]
-    v_items = v_items[HEAD_V:]
-    groups = (("q", 0), ("q", 1), ("k", 0), ("k", 1), ("q", 2), ("q", 3), ("k", 2), ("k", 3))
-    for i, (mat, c) in enumerate(groups):
-        order.extend([(mat, c, g) for g in range(4)])
-        order.extend(v_items[: V_AFTER[i]])
-        v_items = v_items[V_AFTER[i] :]
-    assert not v_items
+    w_items = [(mat, c, g) for (mat, c) in (("q", 0), ("q", 1), ("k", 0), ("k", 1), ("q", 2), ("q", 3), ("k", 2), ("k", 3))
+               for g in range(4)]
+    order = []
+    for ch in PATTERN:
+        if ch == "v":
+            order.append(v_items[0])
+            v_items = v_items[1:]
+        else:
+            order.append(w_items[0])
+            w_items = w_items[1:]
+    assert not v_items and not w_items
     return order
 
 
@@ -78,7 +84,10 @@ def tile_selfattention_kernel(tc, x, Wq, Wk, Wv_bytes, Wv_scale, st_pos, out_0, 
         ctx.enter_context(tc.manual_schedule())
 
         def unit_of(it):
-            return (it[0], it[1] // 2, it[2])
+            mat, c, g = it
+            if (mat, c // 2) in NARROW:
+                return (mat, 512 * c, 512, g)
+            return (mat, 1024 * (c // 2), 1024, g)
 
         need = {}
         for n, it in enumerate(order):
@@ -92,18 +101,18 @@ def tile_selfattention_kernel(tc, x, Wq, Wk, Wv_bytes, Wv_scale, st_pos, out_0, 
         reads_left = {}
 
         def load(u):
-            mat, half, g = u
+            mat, col, width, g = u
             rows = slice(512 * g, 512 * (g + 1))
-            cols = slice(1024 * half, 1024 * (half + 1))
+            cols = slice(col, col + width)
             if mat == "v":
-                t = byt.tile([P, 4, 1024], U8, name="vb")
+                t = byt.tile([P, 4, width], U8, name="vb")
                 src = Wv_bytes
             else:
-                t = raw.tile([P, 4, 1024], BF16, name="rw", align_bytes=64)
+                t = raw.tile([P, 4, width], BF16, name="rw", align_bytes=64)
                 src = weights[mat]
             nc.sync.dma_start(out=t[:], in_=src[rows, cols].rearrange("(p j) n -> p j n", j=4))
             units[u] = t
-            reads_left[u] = 2
+            reads_left[u] = width // 512
             live["v" if mat == "v" else "w"].append(u)
 
         def load_next(kind):
@@ -128,11 +137,11 @@ def tile_selfattention_kernel(tc, x, Wq, Wk, Wv_bytes, Wv_scale, st_pos, out_0, 
         nc.scalar.dma_start(out=vsc[:], in_=Wv_scale.rearrange("(g p j) o -> p g (j o)", p=P, j=4))
         x_sb = raw.tile([P, 2, 2048], BF16, name="rw", align_bytes=64)
         xg = raw.tile([P, 4, 1024], BF16, name="rw", align_bytes=64)
-        for u in (("x", 0, 0), ("x", 1, 0)):
+        for u in (("x", 0, 0, 0), ("x", 1, 0, 0)):
             live["w"].append(u)
             reads_left[u] = 1
-        load_next("v")
-        load_next("v")
+        for kind in FIRST_LOADS:
+            load_next(kind)
         nc.sync.dma_start(out=x_sb[:], in_=x.rearrange("b s d -> s b d"))
 
         ident = const.tile([P, P], F32, name="ident")
@@ -228,7 +237,10 @@ def tile_selfattention_kernel(tc, x, Wq, Wk, Wv_bytes, Wv_scale, st_pos, out_0, 
         for n, it in enumerate(order):
             if it[0] != "v" and (it[0], it[1]) not in group_no:
                 group_no[(it[0], it[1])] = len(group_no)
-            s_inter[n] = it[0] != "v" and it[2] in S_PLAN[group_no[(it[0], it[1])]]
+            if it[0] == "v":
+                s_inter[n] = (it[1], it[2]) in S_VITEMS
+            else:
+                s_inter[n] = it[2] in S_PLAN[group_no[(it[0], it[1])]]
 
         def later(step, fn):
             tasks.setdefault(step, []).append(fn)
@@ -237,7 +249,7 @@ def tile_selfattention_kernel(tc, x, Wq, Wk, Wv_bytes, Wv_scale, st_pos, out_0, 
             mat, c, g = order[n]
             u = unit_of(order[n])
             wd = wide.tile([P, 4, 512], BF16, name="wd")
-            lo = 512 * (c % 2)
+            lo = 512 * c - u[1]
             for j in range(4):
                 nc.scalar.activation(out=wd[:, j, :], in_=units[u][:, j, lo : lo + 512].bitcast(FP8), func=ACT.Copy,
                                      scale=vsc[:, g, j : j + 1])
@@ -250,7 +262,7 @@ def tile_selfattention_kernel(tc, x, Wq, Wk, Wv_bytes, Wv_scale, st_pos, out_0, 
             if mat == "v":
                 src = wd_tiles[n][:]
             else:
-                lo = 512 * (c % 2)
+                lo = 512 * c - unit_of(order[n])[1]
                 src = units[unit_of(order[n])][:, :, lo : lo + 512]
             if FAST_COPY:
                 dst = gr[:].rearrange("p (c i j) -> p c j i", i=4, j=4)
@@ -377,13 +389,13 @@ def tile_selfattention_kernel(tc, x, Wq, Wk, Wv_bytes, Wv_scale, st_pos, out_0, 
             n = step + 1
             if 0 <= n < n_items and not s_inter[n]:
                 inter(n)
-            if step == -1:
+            if step == X_STEP:
                 for g in range(4):
                     x_transpose(g)
-                unit_read(("x", 0, 0))
+                unit_read(("x", 0, 0, 0))
             if 0 <= step < n_items:
                 quant(step, step)
-            if step == 0:
+            if step == X_STEP + 1:
                 x_quant()
-                unit_read(("x", 1, 0))
+                unit_read(("x", 1, 0, 0))
             step += 1

@@ -35,7 +35,6 @@ LAG_T = 2
 LAG_O = 3
 LAG_R = 1
 LAG_V = 2
-S_DIAG = 10
 X_ENG = "V"
 S_PLAN = ((1, 3), (1,), (1, 3), (1,), (1,), (1,), (1,), ())
 FAST_COPY = True
@@ -144,12 +143,12 @@ def tile_selfattention_kernel(tc, x, Wq, Wk, Wv_bytes, Wv_scale, st_pos, out_0, 
             load_next(kind)
         nc.sync.dma_start(out=x_sb[:], in_=x.rearrange("b s d -> s b d"))
 
-        ident = const.tile([P, P], F32, name="ident")
-        make_identity(nc, ident[:])
         pidx = const.tile([P, 1], I32, name="pidx")
         nc.gpsimd.iota(pidx[:], pattern=[[0, 1]], base=0, channel_multiplier=1)
         hidx = const.tile([P, HEADS], I32, name="hidx")
         nc.gpsimd.iota(hidx[:], pattern=[[1, HEADS]], base=0, channel_multiplier=0)
+        ident = const.tile([P, P], F32, name="ident")
+        make_identity(nc, ident[:])
 
         zero = const.tile([P, 1], F32, name="zero")
         nc.vector.memset(zero[:], 0.0)
@@ -161,7 +160,6 @@ def tile_selfattention_kernel(tc, x, Wq, Wk, Wv_bytes, Wv_scale, st_pos, out_0, 
             nc.vector.tensor_scalar(out=bits[:, b : b + 1], in0=pidx[:], scalar1=b, scalar2=1,
                                     op0=ALU.logical_shift_right, op1=ALU.bitwise_and)
         fac = const.tile([P, 7], F32, name="fac")
-        nc.vector.tensor_scalar(out=fac[:, 0:1], in0=bits[:, 0:1], scalar1=-2.0, scalar2=1.0, op0=ALU.mult, op1=ALU.add)
         for b in range(1, 7):
             ratio = ROPE_BASE ** (-(2.0 ** (b - 1)) / 64.0)
             nc.vector.tensor_scalar(out=fac[:, b : b + 1], in0=bits[:, b : b + 1], scalar1=ratio - 1.0, scalar2=1.0,
@@ -172,10 +170,13 @@ def tile_selfattention_kernel(tc, x, Wq, Wk, Wv_bytes, Wv_scale, st_pos, out_0, 
         nc.vector.tensor_tensor(out=th1[:], in0=th3[:, 0:1], in1=th3[:, 1:2], op=ALU.mult)
         theta = const.tile([P, 1], F32, name="theta")
         nc.vector.tensor_tensor(out=theta[:], in0=th1[:], in1=th3[:, 2:3], op=ALU.mult)
+        phase = const.tile([P, 2], F32, name="phase")
+        nc.vector.tensor_scalar(out=phase[:, 0:1], in0=bits[:, 0:1], scalar1=PI / 2, scalar2=PI / 2, op0=ALU.mult, op1=ALU.add)
+        nc.vector.tensor_scalar(out=phase[:, 1:2], in0=bits[:, 0:1], scalar1=PI / 2, scalar2=None, op0=ALU.mult)
         ang = const.tile([P, 2 * HEADS], F32, name="ang")
-        nc.vector.tensor_scalar(out=ang[:, 0:HEADS], in0=hidx[:], scalar1=theta[:, 0:1], scalar2=None, op0=ALU.mult)
-        nc.vector.tensor_scalar(out=ang[:, HEADS : 2 * HEADS], in0=hidx[:], scalar1=theta[:, 0:1], scalar2=PI / 2,
-                                op0=ALU.mult, op1=ALU.add)
+        for e in range(2):
+            nc.vector.tensor_scalar(out=ang[:, HEADS * e : HEADS * (e + 1)], in0=hidx[:], scalar1=theta[:, 0:1],
+                                    scalar2=phase[:, e : e + 1], op0=ALU.mult, op1=ALU.add)
         turn1 = const.tile([P, 2 * HEADS], F32, name="turn1")
         nc.vector.tensor_scalar(out=turn1[:], in0=ang[:], scalar1=PI, scalar2=None, op0=ALU.is_ge)
         turn2 = const.tile([P, 2 * HEADS], F32, name="turn2")
@@ -184,25 +185,16 @@ def tile_selfattention_kernel(tc, x, Wq, Wk, Wv_bytes, Wv_scale, st_pos, out_0, 
         nc.vector.scalar_tensor_tensor(out=turn3[:], in0=ang[:], scalar=5 * PI, in1=turn2[:], op0=ALU.is_ge, op1=ALU.add)
         red = const.tile([P, 2 * HEADS], F32, name="red")
         nc.vector.scalar_tensor_tensor(out=red[:], in0=turn3[:], scalar=-2 * PI, in1=ang[:], op0=ALU.mult, op1=ALU.add)
-        sc = const.tile([P, 2 * HEADS], F32, name="sc")
-        nc.scalar.activation(out=sc[:], in_=red[:], func=ACT.Sin)
-        ssin = const.tile([P, HEADS], F32, name="ssin")
-        nc.vector.tensor_scalar(out=ssin[:], in0=sc[:, 0:HEADS], scalar1=fac[:, 0:1], scalar2=None, op0=ALU.mult)
-        swp = const.tile([P, P], F32, name="swp")
-        swp_v = swp[:].rearrange("p (i e) -> p i e", e=2)
+        entry = const.tile([P, 2 * HEADS], F32, name="entry")
+        nc.scalar.activation(out=entry[:], in_=red[:], func=ACT.Sin)
+        pairs = const.tile([P, P // 2], F32, name="pairs")
         id_v = ident[:].rearrange("p (i e) -> p i e", e=2)
-        nc.vector.tensor_copy(out=swp_v[:, :, 0:1], in_=id_v[:, :, 1:2])
-        nc.vector.tensor_copy(out=swp_v[:, :, 1:2], in_=id_v[:, :, 0:1])
+        nc.vector.tensor_tensor(out=pairs[:].unsqueeze(2), in0=id_v[:, :, 0:1], in1=id_v[:, :, 1:2], op=ALU.add)
         rmat = const.tile([P, HEADS, P], F32, name="rmat")
-        for h in range(HEADS):
-            if h < S_DIAG:
-                nc.scalar.activation(out=rmat[:, h, :], in_=ident[:], func=ACT.Copy, scale=sc[:, HEADS + h : HEADS + h + 1])
-            else:
-                nc.vector.tensor_scalar(out=rmat[:, h, :], in0=ident[:], scalar1=sc[:, HEADS + h : HEADS + h + 1], scalar2=None,
-                                        op0=ALU.mult)
-        for h in range(HEADS):
-            nc.vector.scalar_tensor_tensor(out=rmat[:, h, :], in0=swp[:], scalar=ssin[:, h : h + 1], in1=rmat[:, h, :],
-                                           op0=ALU.mult, op1=ALU.add)
+        full = [P, HEADS, P // 2, 2]
+        nc.vector.tensor_tensor(out=rmat[:].rearrange("p h (i e) -> p h i e", e=2),
+                                in0=pairs[:].unsqueeze(1).unsqueeze(3).to_broadcast(full),
+                                in1=entry[:].rearrange("p (e h) -> p h e", e=2).unsqueeze(2).to_broadcast(full), op=ALU.mult)
 
         def evac(eng, dst, src):
             if eng == "S":

@@ -36,7 +36,11 @@ LAG_O = 3
 LAG_R = 1
 LAG_V = 2
 X_ENG = "V"
-S_PLAN = ((1, 3), (1,), (1, 3), (1,), (1,), (1,), (1,), ())
+S_PLAN = ((1, 3), (3,), (3,), (), (1,), (3,), (), ())
+T_PLAN = ((), (1,), (1,), (1,), (), (1,), (1,), ())
+LEAD_T = 6
+DEFER = (1, 2)
+LAG_B = 3
 FAST_COPY = True
 PATTERN = "vvvvv" + "wwwwv" * 7 + "wwwwvvvv"
 FAST_END = 8
@@ -88,10 +92,23 @@ def tile_selfattention_kernel(tc, x, Wq, Wk, Wv_bytes, Wv_scale, st_pos, out_0, 
                 return (mat, 512 * c, 512, g)
             return (mat, 1024 * (c // 2), 1024, g)
 
+        s_inter = {}
+        t_inter = {}
+        group_no = {}
+        for n, it in enumerate(order):
+            if it[0] != "v" and (it[0], it[1]) not in group_no:
+                group_no[(it[0], it[1])] = len(group_no)
+            if it[0] == "v":
+                s_inter[n] = (it[1], it[2]) in S_VITEMS
+                t_inter[n] = False
+            else:
+                s_inter[n] = it[2] in S_PLAN[group_no[(it[0], it[1])]]
+                t_inter[n] = it[2] in T_PLAN[group_no[(it[0], it[1])]]
+
         need = {}
         for n, it in enumerate(order):
             if unit_of(it) not in need:
-                need[unit_of(it)] = n - (LEAD_WIDEN if it[0] == "v" else LEAD_SINT)
+                need[unit_of(it)] = n - (LEAD_WIDEN if it[0] == "v" else (LEAD_T if t_inter[n] else LEAD_SINT))
         load_list = sorted(need, key=lambda u: need[u])
         room = {"v": N_BYT, "w": N_RAW}
         pending = {"v": [u for u in load_list if u[0] == "v"], "w": [u for u in load_list if u[0] != "v"]}
@@ -149,6 +166,8 @@ def tile_selfattention_kernel(tc, x, Wq, Wk, Wv_bytes, Wv_scale, st_pos, out_0, 
         nc.gpsimd.iota(hidx[:], pattern=[[1, HEADS]], base=0, channel_multiplier=0)
         ident = const.tile([P, P], F32, name="ident")
         make_identity(nc, ident[:])
+        ident_b = const.tile([P, P], BF16, name="ident_b")
+        make_identity(nc, ident_b[:])
 
         zero = const.tile([P, 1], F32, name="zero")
         nc.vector.memset(zero[:], 0.0)
@@ -224,15 +243,6 @@ def tile_selfattention_kernel(tc, x, Wq, Wk, Wv_bytes, Wv_scale, st_pos, out_0, 
         code = {}
         acc = {}
         tasks = {}
-        s_inter = {}
-        group_no = {}
-        for n, it in enumerate(order):
-            if it[0] != "v" and (it[0], it[1]) not in group_no:
-                group_no[(it[0], it[1])] = len(group_no)
-            if it[0] == "v":
-                s_inter[n] = (it[1], it[2]) in S_VITEMS
-            else:
-                s_inter[n] = it[2] in S_PLAN[group_no[(it[0], it[1])]]
 
         def later(step, fn):
             tasks.setdefault(step, []).append(fn)
@@ -267,11 +277,43 @@ def tile_selfattention_kernel(tc, x, Wq, Wk, Wv_bytes, Wv_scale, st_pos, out_0, 
             if mat != "v":
                 unit_read(unit_of(order[n]))
 
+        il_tiles = {}
+
+        def pe_inter(n):
+            mat, c, g = order[n]
+            u = unit_of(order[n])
+            lo = 512 * c - u[1]
+            for hf in range(2):
+                il = psum.tile([P, 1024], BF16, name="aux", bufs=2)
+                for q in range(2):
+                    col = lo + 256 * hf + 128 * q
+                    nc.tensor.matmul(out=il[:, 512 * q : 512 * (q + 1)].rearrange("p (c j) -> p c j", j=4), lhsT=ident_b[:],
+                                     rhs=units[u][:, :, col : col + 128].rearrange("p j c -> p c j"), start=True, stop=True)
+                il_tiles[(n, hf)] = il
+            unit_read(u)
+
+        def pe_inter_out(n):
+            gr = grp.tile([P, 2048], BF16, name="gr", align_bytes=64)
+            for hf in range(2):
+                nc.scalar.copy(out=gr[:, 1024 * hf : 1024 * (hf + 1)], in_=il_tiles[(n, hf)][:])
+            gr_tiles[n] = gr
+
+        v_codes = {}
+
+        def v_burst(c):
+            for t in range(2):
+                acc[t] = psum.tile([P, 512], F32, name="aux", bufs=2)
+                for g in range(4):
+                    cv, sv = v_codes[(c, g)]
+                    nc.tensor.matmul_mx(out=acc[t][:], lhsT=xq[:, g, 128 * t : 128 * (t + 1)].bitcast(FP8X4),
+                                        lhsT_scale=xs[:, g, 128 * t : 128 * (t + 1)], rhs=cv[:].bitcast(FP8X4), rhs_scale=sv[:],
+                                        start=(g == 0), stop=(g == 3))
+
         def v_matmul(n, cv, sv):
             mat, c, g = order[n]
             for t in range(2):
                 if g == 0:
-                    acc[t] = psum.tile([P, 512], F32, name="acc", bufs=2)
+                    acc[t] = psum.tile([P, 512], F32, name="aux", bufs=2)
                 nc.tensor.matmul_mx(out=acc[t][:], lhsT=xq[:, g, 128 * t : 128 * (t + 1)].bitcast(FP8X4),
                                     lhsT_scale=xs[:, g, 128 * t : 128 * (t + 1)], rhs=cv[:].bitcast(FP8X4), rhs_scale=sv[:],
                                     start=(g == 0), stop=(g == 3))
@@ -350,10 +392,15 @@ def tile_selfattention_kernel(tc, x, Wq, Wk, Wv_bytes, Wv_scale, st_pos, out_0, 
                 cv = codv.tile([P, 512], U32, name="cv", align_bytes=64)
                 sv = codv.tile([P, 512], U8, name="sv", align_bytes=64)
                 nc.vector.quantize_mx(out=cv[:].bitcast(FP8X4), scales=sv[:], in_=gr_tiles[n][:])
-                later(step + 1, lambda: v_matmul(n, cv, sv))
+                if c in DEFER:
+                    v_codes[(c, g)] = (cv, sv)
+                    if g == 3:
+                        later(step + 1, lambda: v_burst(c))
+                else:
+                    later(step + 1, lambda: v_matmul(n, cv, sv))
                 if g == 3:
                     last = n == n_items - 1
-                    later(step + (1 if last else LAG_V), lambda: v_out(c, ("S", "V") if last else ("S", "S")))
+                    later(step + (1 if last else (LAG_B if c in DEFER else LAG_V)), lambda: v_out(c, ("S", "V") if last else ("S", "S")))
                 return
             if g == 0:
                 cq_new = cod.tile([P, 4, 512], U32, name="cq", align_bytes=64)
@@ -375,11 +422,16 @@ def tile_selfattention_kernel(tc, x, Wq, Wk, Wv_bytes, Wv_scale, st_pos, out_0, 
             n = step + LEAD_WIDEN
             if 0 <= n < n_items and order[n][0] == "v":
                 widen(n)
+            n = step + LEAD_T
+            if 0 <= n < n_items and t_inter[n]:
+                pe_inter(n)
             n = step + LEAD_SINT
             if 0 <= n < n_items and s_inter[n]:
                 inter(n)
+            if 0 <= n < n_items and t_inter[n]:
+                pe_inter_out(n)
             n = step + 1
-            if 0 <= n < n_items and not s_inter[n]:
+            if 0 <= n < n_items and not s_inter[n] and not t_inter[n]:
                 inter(n)
             if step == X_STEP:
                 for g in range(4):

@@ -42,6 +42,7 @@ LEAD_T = 6
 DEFER = (1, 2)
 LAG_B = 3
 FAST_COPY = True
+RUN = 2
 PATTERN = "vvvvv" + "wwwwv" * 7 + "wwwwvvvv"
 FAST_END = 8
 NARROW = (("v", 0),)
@@ -267,8 +268,8 @@ def tile_selfattention_kernel(tc, x, Wq, Wk, Wv_bytes, Wv_scale, st_pos, out_0, 
                 lo = 512 * c - unit_of(order[n])[1]
                 src = units[unit_of(order[n])][:, :, lo : lo + 512]
             if FAST_COPY:
-                dst = gr[:].rearrange("p (c i j) -> p c j i", i=4, j=4)
-                src = src.rearrange("p j (c i) -> p c j i", i=4)
+                dst = gr[:].rearrange("p (c i j) -> p c j i", i=RUN, j=4)
+                src = src.rearrange("p j (c i) -> p c j i", i=RUN)
             else:
                 dst = gr[:].rearrange("p (n j) -> p n j", j=4)
                 src = src.rearrange("p j n -> p n j")

@@ -1,3 +1,4 @@
+import math
 from contextlib import ExitStack
 
 import concourse.mybir as mybir
@@ -31,30 +32,27 @@ N_OUT = 8
 LEAD_WIDEN = 5
 LOAD_LEAD = 10
 LEAD_SINT = 3
+LEAD_T = 6
 LAG_T = 2
 LAG_O = 3
 LAG_R = 1
 LAG_V = 2
-X_ENG = "V"
-S_PLAN = ((1, 3), (3,), (3,), (), (1,), (3,), (), ())
-T_PLAN = ((), (1,), (1,), (1,), (), (1,), (1,), ())
-LEAD_T = 6
-DEFER = (1, 2)
 LAG_B = 3
-FAST_COPY = True
+X_ENG = "V"
 RUN = 2
-PATTERN = "vvvvv" + "wwwwv" * 7 + "wwwwvvvv"
 FAST_END = 8
 NARROW = (("v", 0),)
-S_VITEMS = ()
 FIRST_LOADS = ("v", "v")
 X_STEP = -1
+W_GROUPS = (("q", 0, 512, "VSVS"), ("q", 512, 512, "VTVH"), ("k", 0, 512, "VTVH"), ("k", 512, 512, "VTVH"), ("q", 1024, 512, "VSVH"),
+            ("q", 1536, 512, "VTVH"), ("k", 1024, 512, "VTVV"), ("k", 1536, 512, "VVVV"))
+V_CHUNKS = ((0, 512, False), (512, 512, True), (1024, 512, True), (1536, 512, False))
+PATTERN = "vvvvv" + "wwwwv" * 7 + "wwwwvvvv"
 
 
 def build_order():
-    v_items = [("v", c, g) for c in range(4) for g in range(4)]
-    w_items = [(mat, c, g) for (mat, c) in (("q", 0), ("q", 1), ("k", 0), ("k", 1), ("q", 2), ("q", 3), ("k", 2), ("k", 3))
-               for g in range(4)]
+    v_items = [("v", col, width, g) for (col, width, at_once) in V_CHUNKS for g in range(4)]
+    w_items = [(mat, col, width, g) for (mat, col, width, plan) in W_GROUPS for g in range(4)]
     order = []
     for ch in PATTERN:
         if ch == "v":
@@ -87,29 +85,48 @@ def tile_selfattention_kernel(tc, x, Wq, Wk, Wv_bytes, Wv_scale, st_pos, out_0, 
         psum = ctx.enter_context(tc.psum_pool(name="psum", bufs=3))
         ctx.enter_context(tc.manual_schedule())
 
-        def unit_of(it):
-            mat, c, g = it
-            if (mat, c // 2) in NARROW:
-                return (mat, 512 * c, 512, g)
-            return (mat, 1024 * (c // 2), 1024, g)
-
-        s_inter = {}
-        t_inter = {}
-        group_no = {}
+        plans = {}
+        for (mat, col, width, plan) in W_GROUPS:
+            plans[(mat, col)] = plan
+        at_once = {}
+        for (col, width, flag) in V_CHUNKS:
+            at_once[col] = flag
+        mode = {}
         for n, it in enumerate(order):
-            if it[0] != "v" and (it[0], it[1]) not in group_no:
-                group_no[(it[0], it[1])] = len(group_no)
+            mode[n] = "V" if it[0] == "v" else plans[(it[0], it[1])][it[3]]
+            assert mode[n] in ("V", "S") or it[2] == 512
+
+        tpos = {}
+        for n, it in enumerate(order):
+            tpos[n] = sum([o[2] for o in order[:n]]) / 512.0
+
+        def step_for(n, lead):
+            target = tpos[n] - lead
+            if target < 0:
+                return int(math.floor(target))
+            return max([m for m in range(n_items) if tpos[m] <= target])
+
+        widen_at = {}
+        pe_at = {}
+        s_at = {}
+        for n, it in enumerate(order):
             if it[0] == "v":
-                s_inter[n] = (it[1], it[2]) in S_VITEMS
-                t_inter[n] = False
-            else:
-                s_inter[n] = it[2] in S_PLAN[group_no[(it[0], it[1])]]
-                t_inter[n] = it[2] in T_PLAN[group_no[(it[0], it[1])]]
+                widen_at.setdefault(step_for(n, LEAD_WIDEN), []).append(n)
+            if mode[n] == "T":
+                pe_at.setdefault(step_for(n, LEAD_T), []).append(n)
+            if mode[n] in ("S", "T", "H"):
+                s_at.setdefault(step_for(n, LEAD_SINT), []).append(n)
+
+        def unit_of(it):
+            mat, col, width, g = it
+            if (mat, col // 1024) in NARROW:
+                return (mat, 512 * (col // 512), 512, g)
+            return (mat, 1024 * (col // 1024), 1024, g)
 
         need = {}
         for n, it in enumerate(order):
             if unit_of(it) not in need:
-                need[unit_of(it)] = n - (LEAD_WIDEN if it[0] == "v" else (LEAD_T if t_inter[n] else LEAD_SINT))
+                need[unit_of(it)] = step_for(n, LEAD_WIDEN if it[0] == "v" else (LEAD_T if mode[n] == "T" else LEAD_SINT))
         load_list = sorted(need, key=lambda u: need[u])
         room = {"v": N_BYT, "w": N_RAW}
         pending = {"v": [u for u in load_list if u[0] == "v"], "w": [u for u in load_list if u[0] != "v"]}
@@ -129,7 +146,7 @@ def tile_selfattention_kernel(tc, x, Wq, Wk, Wv_bytes, Wv_scale, st_pos, out_0, 
                 src = weights[mat]
             nc.sync.dma_start(out=t[:], in_=src[rows, cols].rearrange("(p j) n -> p j n", j=4))
             units[u] = t
-            reads_left[u] = width // 512
+            reads_left[u] = len([it for it in order if unit_of(it) == u])
             live["v" if mat == "v" else "w"].append(u)
 
         def load_next(kind):
@@ -249,47 +266,46 @@ def tile_selfattention_kernel(tc, x, Wq, Wk, Wv_bytes, Wv_scale, st_pos, out_0, 
             tasks.setdefault(step, []).append(fn)
 
         def widen(n):
-            mat, c, g = order[n]
+            mat, col, width, g = order[n]
             u = unit_of(order[n])
-            wd = wide.tile([P, 4, 512], BF16, name="wd")
-            lo = 512 * c - u[1]
+            wd = wide.tile([P, 4, width], BF16, name="wd")
+            lo = col - u[1]
             for j in range(4):
-                nc.scalar.activation(out=wd[:, j, :], in_=units[u][:, j, lo : lo + 512].bitcast(FP8), func=ACT.Copy,
+                nc.scalar.activation(out=wd[:, j, :], in_=units[u][:, j, lo : lo + width].bitcast(FP8), func=ACT.Copy,
                                      scale=vsc[:, g, j : j + 1])
             wd_tiles[n] = wd
             unit_read(u)
 
-        def inter(n):
-            mat, c, g = order[n]
-            gr = grp.tile([P, 2048], BF16, name="gr", align_bytes=64)
+        def inter(n, eng, part=None):
+            mat, col, width, g = order[n]
+            if part != 1:
+                gr_new = grp.tile([P, 4 * width], BF16, name="gr", align_bytes=64)
+                gr_tiles[n] = gr_new
+            gr = gr_tiles[n]
             if mat == "v":
                 src = wd_tiles[n][:]
             else:
-                lo = 512 * c - unit_of(order[n])[1]
-                src = units[unit_of(order[n])][:, :, lo : lo + 512]
-            if FAST_COPY:
-                dst = gr[:].rearrange("p (c i j) -> p c j i", i=RUN, j=4)
-                src = src.rearrange("p j (c i) -> p c j i", i=RUN)
-            else:
-                dst = gr[:].rearrange("p (n j) -> p n j", j=4)
-                src = src.rearrange("p j n -> p n j")
-            evac("S" if s_inter[n] else "V", dst, src)
-            gr_tiles[n] = gr
-            if mat != "v":
+                lo = col - unit_of(order[n])[1]
+                src = units[unit_of(order[n])][:, :, lo : lo + width]
+            dst = gr[:]
+            if part is not None:
+                src = src[:, :, (width // 2) * part : (width // 2) * (part + 1)]
+                dst = gr[:, 2 * width * part : 2 * width * (part + 1)]
+            evac(eng, dst.rearrange("p (c i j) -> p c j i", i=RUN, j=4), src.rearrange("p j (c i) -> p c j i", i=RUN))
+            if mat != "v" and part != 0:
                 unit_read(unit_of(order[n]))
 
         il_tiles = {}
 
         def pe_inter(n):
-            mat, c, g = order[n]
+            mat, col, width, g = order[n]
             u = unit_of(order[n])
-            lo = 512 * c - u[1]
             for hf in range(2):
                 il = psum.tile([P, 1024], BF16, name="aux", bufs=2)
                 for q in range(2):
-                    col = lo + 256 * hf + 128 * q
+                    lo = col - u[1] + 256 * hf + 128 * q
                     nc.tensor.matmul(out=il[:, 512 * q : 512 * (q + 1)].rearrange("p (c j) -> p c j", j=4), lhsT=ident_b[:],
-                                     rhs=units[u][:, :, col : col + 128].rearrange("p j c -> p c j"), start=True, stop=True)
+                                     rhs=units[u][:, :, lo : lo + 128].rearrange("p j c -> p c j"), start=True, stop=True)
                 il_tiles[(n, hf)] = il
             unit_read(u)
 
@@ -301,29 +317,29 @@ def tile_selfattention_kernel(tc, x, Wq, Wk, Wv_bytes, Wv_scale, st_pos, out_0, 
 
         v_codes = {}
 
-        def v_burst(c):
+        def v_pass(t, g, cv, sv):
+            nc.tensor.matmul_mx(out=acc[t][:], lhsT=xq[:, g, 128 * t : 128 * (t + 1)].bitcast(FP8X4),
+                                lhsT_scale=xs[:, g, 128 * t : 128 * (t + 1)], rhs=cv[:].bitcast(FP8X4), rhs_scale=sv[:],
+                                start=(g == 0), stop=(g == 3))
+
+        def v_burst(col, width):
             for t in range(2):
-                acc[t] = psum.tile([P, 512], F32, name="aux", bufs=2)
+                acc[t] = psum.tile([P, width], F32, name="aux", bufs=2)
                 for g in range(4):
-                    cv, sv = v_codes[(c, g)]
-                    nc.tensor.matmul_mx(out=acc[t][:], lhsT=xq[:, g, 128 * t : 128 * (t + 1)].bitcast(FP8X4),
-                                        lhsT_scale=xs[:, g, 128 * t : 128 * (t + 1)], rhs=cv[:].bitcast(FP8X4), rhs_scale=sv[:],
-                                        start=(g == 0), stop=(g == 3))
+                    v_pass(t, g, v_codes[(col, g)][0], v_codes[(col, g)][1])
 
         def v_matmul(n, cv, sv):
-            mat, c, g = order[n]
+            mat, col, width, g = order[n]
             for t in range(2):
                 if g == 0:
-                    acc[t] = psum.tile([P, 512], F32, name="aux", bufs=2)
-                nc.tensor.matmul_mx(out=acc[t][:], lhsT=xq[:, g, 128 * t : 128 * (t + 1)].bitcast(FP8X4),
-                                    lhsT_scale=xs[:, g, 128 * t : 128 * (t + 1)], rhs=cv[:].bitcast(FP8X4), rhs_scale=sv[:],
-                                    start=(g == 0), stop=(g == 3))
+                    acc[t] = psum.tile([P, width], F32, name="aux", bufs=2)
+                v_pass(t, g, cv, sv)
 
-        def v_out(c, engs):
+        def v_out(col, width, engs):
             for t in range(2):
-                ot = outp.tile([P, 512], F32, name="ot")
+                ot = outp.tile([P, width], F32, name="ot")
                 evac(engs[t], ot[:], acc[t][:])
-                nc.sync.dma_start(out=out_2[t].rearrange("s h d -> s (h d)")[:, 512 * c : 512 * (c + 1)], in_=ot[:])
+                nc.sync.dma_start(out=out_2[t].rearrange("s h d -> s (h d)")[:, col : col + width], in_=ot[:])
 
         head_queue = []
         multiplied = []
@@ -332,8 +348,8 @@ def tile_selfattention_kernel(tc, x, Wq, Wk, Wv_bytes, Wv_scale, st_pos, out_0, 
         slot = [0]
 
         def head_matmul(hd):
-            mat, c, hh = hd["mat"], hd["c"], hd["hh"]
-            cq, sq = code[(mat, c)]
+            cq, sq = code[(hd["mat"], hd["col"])]
+            hh = hd["hh"]
             tt = psum.tile([P, 256], F32, name="tT")
             for g in range(4):
                 nc.tensor.matmul_mx(out=tt[:], lhsT=cq[:, g, 128 * hh : 128 * (hh + 1)].bitcast(FP8X4),
@@ -351,12 +367,12 @@ def tile_selfattention_kernel(tc, x, Wq, Wk, Wv_bytes, Wv_scale, st_pos, out_0, 
             hl = hd["hh"] % 2
             for t in range(2):
                 nc.tensor.matmul(out=pair_tile[:, 256 * t + 128 * hl : 256 * t + 128 * (hl + 1)],
-                                 lhsT=ts[:, 128 * t : 128 * (t + 1)], rhs=rmat[:, 4 * hd["c"] + hd["hh"], :], start=True, stop=True)
+                                 lhsT=ts[:, 128 * t : 128 * (t + 1)], rhs=rmat[:, hd["col"] // 128 + hd["hh"], :], start=True, stop=True)
 
         def pair_out(hd, pair_tile, eng):
             ot = outp.tile([P, 512], F32, name="ot")
             evac(eng, ot[:], pair_tile[:])
-            lo = 512 * hd["c"] + 128 * (hd["hh"] - 1)
+            lo = hd["col"] + 128 * (hd["hh"] - 1)
             nc.sync.dma_start(out=outs[hd["mat"]].rearrange("b s h d -> s b (h d)")[:, :, lo : lo + 256],
                               in_=ot[:].rearrange("p (t n) -> p t n", t=2))
 
@@ -388,52 +404,60 @@ def tile_selfattention_kernel(tc, x, Wq, Wk, Wv_bytes, Wv_scale, st_pos, out_0, 
                     rotated.append((hd, pair_now[0], slot[0]))
 
         def quant(n, step):
-            mat, c, g = order[n]
+            mat, col, width, g = order[n]
             if mat == "v":
-                cv = codv.tile([P, 512], U32, name="cv", align_bytes=64)
-                sv = codv.tile([P, 512], U8, name="sv", align_bytes=64)
+                cv = codv.tile([P, width], U32, name="cv", align_bytes=64)
+                sv = codv.tile([P, width], U8, name="sv", align_bytes=64)
                 nc.vector.quantize_mx(out=cv[:].bitcast(FP8X4), scales=sv[:], in_=gr_tiles[n][:])
-                if c in DEFER:
-                    v_codes[(c, g)] = (cv, sv)
+                if at_once[col]:
+                    v_codes[(col, g)] = (cv, sv)
                     if g == 3:
-                        later(step + 1, lambda: v_burst(c))
+                        later(step + 1, lambda: v_burst(col, width))
                 else:
                     later(step + 1, lambda: v_matmul(n, cv, sv))
                 if g == 3:
                     last = n == n_items - 1
-                    later(step + (1 if last else (LAG_B if c in DEFER else LAG_V)), lambda: v_out(c, ("S", "V") if last else ("S", "S")))
+                    later(step + (1 if last else (LAG_B if at_once[col] else LAG_V)),
+                          lambda: v_out(col, width, ("S", "V") if last else ("S", "S")))
                 return
             if g == 0:
-                cq_new = cod.tile([P, 4, 512], U32, name="cq", align_bytes=64)
-                sq_new = cod.tile([P, 4, 512], U8, name="sq", align_bytes=64)
-                code[(mat, c)] = (cq_new, sq_new)
-            cq, sq = code[(mat, c)]
+                cq_new = cod.tile([P, 4, width], U32, name="cq", align_bytes=64)
+                sq_new = cod.tile([P, 4, width], U8, name="sq", align_bytes=64)
+                code[(mat, col)] = (cq_new, sq_new)
+            cq, sq = code[(mat, col)]
             nc.vector.quantize_mx(out=cq[:, g, :].bitcast(FP8X4), scales=sq[:, g, :], in_=gr_tiles[n][:])
             if g == 3:
-                for hh in range(4):
-                    head_queue.append({"mat": mat, "c": c, "hh": hh})
+                for hh in range(width // 128):
+                    head_queue.append({"mat": mat, "col": col, "hh": hh})
 
+        credit = [0.0]
         step = -LEAD_WIDEN - 1
         while step < n_items + 2 or head_queue or multiplied or emptied or rotated:
             issue_loads(step)
-            for rep in range(2 if step >= n_items - FAST_END else 1):
+            share = order[step][2] / 512.0 if 0 <= step < n_items else 1.0
+            fast = step >= n_items or (step >= 0 and tpos[step] >= tpos[n_items - 1] + order[n_items - 1][2] / 512.0 - FAST_END)
+            credit[0] += share * (2 if fast else 1)
+            while credit[0] >= 1:
+                credit[0] -= 1
                 epilogue_slot(step >= n_items)
             for fn in tasks.get(step, []):
                 fn()
-            n = step + LEAD_WIDEN
-            if 0 <= n < n_items and order[n][0] == "v":
+            for n in widen_at.get(step, []):
                 widen(n)
-            n = step + LEAD_T
-            if 0 <= n < n_items and t_inter[n]:
+            for n in pe_at.get(step, []):
                 pe_inter(n)
-            n = step + LEAD_SINT
-            if 0 <= n < n_items and s_inter[n]:
-                inter(n)
-            if 0 <= n < n_items and t_inter[n]:
-                pe_inter_out(n)
+            for n in s_at.get(step, []):
+                if mode[n] == "S":
+                    inter(n, "S")
+                elif mode[n] == "H":
+                    inter(n, "S", 0)
+                else:
+                    pe_inter_out(n)
             n = step + 1
-            if 0 <= n < n_items and not s_inter[n] and not t_inter[n]:
-                inter(n)
+            if 0 <= n < n_items and mode[n] == "H":
+                inter(n, "V", 1)
+            if 0 <= n < n_items and mode[n] == "V":
+                inter(n, "V")
             if step == X_STEP:
                 for g in range(4):
                     x_transpose(g)

@@ -44,6 +44,8 @@ FAST_END = 8
 NARROW = (("v", 0),)
 FIRST_LOADS = ("v", "v")
 X_STEP = -1
+V_WIDENS = 1
+LEAD_VW = 2
 W_GROUPS = (("q", 0, 512, "VSVS"), ("q", 512, 512, "VTVH"), ("k", 0, 512, "VTVH"), ("k", 512, 512, "VTVH"), ("q", 1024, 512, "VSVH"),
             ("q", 1536, 512, "VTVH"), ("k", 1024, 512, "VTVV"), ("k", 1536, 512, "VVVV"))
 V_CHUNKS = ((0, 512, False), (512, 512, True), (1024, 512, True), (1536, 512, False))
@@ -111,7 +113,7 @@ def tile_selfattention_kernel(tc, x, Wq, Wk, Wv_bytes, Wv_scale, st_pos, out_0, 
         s_at = {}
         for n, it in enumerate(order):
             if it[0] == "v":
-                widen_at.setdefault(step_for(n, LEAD_WIDEN), []).append(n)
+                widen_at.setdefault(step_for(n, LEAD_VW if n >= n_items - V_WIDENS else LEAD_WIDEN), []).append(n)
             if mode[n] == "T":
                 pe_at.setdefault(step_for(n, LEAD_T), []).append(n)
             if mode[n] in ("S", "T", "H"):
@@ -271,8 +273,12 @@ def tile_selfattention_kernel(tc, x, Wq, Wk, Wv_bytes, Wv_scale, st_pos, out_0, 
             wd = wide.tile([P, 4, width], BF16, name="wd")
             lo = col - u[1]
             for j in range(4):
-                nc.scalar.activation(out=wd[:, j, :], in_=units[u][:, j, lo : lo + width].bitcast(FP8), func=ACT.Copy,
-                                     scale=vsc[:, g, j : j + 1])
+                if n >= n_items - V_WIDENS:
+                    nc.vector.tensor_scalar(out=wd[:, j, :], in0=units[u][:, j, lo : lo + width].bitcast(FP8), scalar1=vsc[:, g, j : j + 1],
+                                            scalar2=None, op0=ALU.mult)
+                else:
+                    nc.scalar.activation(out=wd[:, j, :], in_=units[u][:, j, lo : lo + width].bitcast(FP8), func=ACT.Copy,
+                                         scale=vsc[:, g, j : j + 1])
             wd_tiles[n] = wd
             unit_read(u)
 

@@ -46,8 +46,7 @@ FIRST_LOADS = ("v", "v")
 X_STEP = -1
 V_WIDENS = 1
 LEAD_VW = 2
-W_GROUPS = (("q", 0, 512, "VSVS"), ("q", 512, 512, "VTVH"), ("k", 0, 512, "VTVH"), ("k", 512, 512, "VTVH"), ("q", 1024, 512, "VSVH"),
-            ("q", 1536, 512, "VTVH"), ("k", 1024, 512, "VTVV"), ("k", 1536, 512, "VVVV"))
+W_GROUPS = (("q", 0, 512, "VSVS"), ("q", 512, 512, "VTVS"), ("k", 0, 512, "VTVH"), ("k", 512, 512, "VTVH"), ("q", 1024, 512, "VSVH"), ("q", 1536, 512, "VTVH"), ("k", 1024, 512, "VTVV"), ("k", 1536, 512, "VVVV"))
 V_CHUNKS = ((0, 512, False), (512, 512, True), (1024, 512, True), (1536, 512, False))
 PATTERN = "vvvvv" + "wwwwv" * 7 + "wwwwvvvv"
 

@@ -46,7 +46,7 @@ FIRST_LOADS = ("v", "v")
 X_STEP = -1
 V_WIDENS = 1
 LEAD_VW = 2
-W_GROUPS = (("q", 0, 512, "VSVS"), ("q", 512, 512, "VTVS"), ("k", 0, 512, "VTVH"), ("k", 512, 512, "VTVH"), ("q", 1024, 512, "VSVH"), ("q", 1536, 512, "VTVH"), ("k", 1024, 512, "VTVV"), ("k", 1536, 512, "VVVV"))
+W_GROUPS = (("q", 0, 512, "VSVS"), ("q", 512, 512, "VTVS"), ("k", 0, 512, "VTVH"), ("k", 512, 512, "VTVH"), ("q", 1024, 512, "VSVH"), ("q", 1536, 512, "VTVH"), ("k", 1024, 512, "VTVV"), ("k", 1536, 512, "VUVV"))
 V_CHUNKS = ((0, 512, False), (512, 512, True), (1024, 512, True), (1536, 512, False))
 PATTERN = "vvvvv" + "wwwwv" * 7 + "wwwwvvvv"
 
@@ -113,9 +113,9 @@ def tile_selfattention_kernel(tc, x, Wq, Wk, Wv_bytes, Wv_scale, st_pos, out_0, 
         for n, it in enumerate(order):
             if it[0] == "v":
                 widen_at.setdefault(step_for(n, LEAD_VW if n >= n_items - V_WIDENS else LEAD_WIDEN), []).append(n)
-            if mode[n] == "T":
+            if mode[n] in ("T", "U"):
                 pe_at.setdefault(step_for(n, LEAD_T), []).append(n)
-            if mode[n] in ("S", "T", "H"):
+            if mode[n] in ("S", "T", "H", "U"):
                 s_at.setdefault(step_for(n, LEAD_SINT), []).append(n)
 
         def unit_of(it):
@@ -127,7 +127,7 @@ def tile_selfattention_kernel(tc, x, Wq, Wk, Wv_bytes, Wv_scale, st_pos, out_0, 
         need = {}
         for n, it in enumerate(order):
             if unit_of(it) not in need:
-                need[unit_of(it)] = step_for(n, LEAD_WIDEN if it[0] == "v" else (LEAD_T if mode[n] == "T" else LEAD_SINT))
+                need[unit_of(it)] = step_for(n, LEAD_WIDEN if it[0] == "v" else (LEAD_T if mode[n] in ("T", "U") else LEAD_SINT))
         load_list = sorted(need, key=lambda u: need[u])
         room = {"v": N_BYT, "w": N_RAW}
         pending = {"v": [u for u in load_list if u[0] == "v"], "w": [u for u in load_list if u[0] != "v"]}
@@ -305,18 +305,19 @@ def tile_selfattention_kernel(tc, x, Wq, Wk, Wv_bytes, Wv_scale, st_pos, out_0, 
         def pe_inter(n):
             mat, col, width, g = order[n]
             u = unit_of(order[n])
-            for hf in range(2):
+            for hf in range(1 if mode[n] == "U" else 2):
                 il = psum.tile([P, 1024], BF16, name="aux", bufs=2)
                 for q in range(2):
                     lo = col - u[1] + 256 * hf + 128 * q
                     nc.tensor.matmul(out=il[:, 512 * q : 512 * (q + 1)].rearrange("p (c j) -> p c j", j=4), lhsT=ident_b[:],
                                      rhs=units[u][:, :, lo : lo + 128].rearrange("p j c -> p c j"), start=True, stop=True)
                 il_tiles[(n, hf)] = il
-            unit_read(u)
+            if mode[n] == "T":
+                unit_read(u)
 
         def pe_inter_out(n):
             gr = grp.tile([P, 2048], BF16, name="gr", align_bytes=64)
-            for hf in range(2):
+            for hf in range(1 if mode[n] == "U" else 2):
                 nc.scalar.copy(out=gr[:, 1024 * hf : 1024 * (hf + 1)], in_=il_tiles[(n, hf)][:])
             gr_tiles[n] = gr
 
@@ -459,7 +460,7 @@ def tile_selfattention_kernel(tc, x, Wq, Wk, Wv_bytes, Wv_scale, st_pos, out_0, 
                 else:
                     pe_inter_out(n)
             n = step + 1
-            if 0 <= n < n_items and mode[n] == "H":
+            if 0 <= n < n_items and mode[n] in ("H", "U"):
                 inter(n, "V", 1)
             if 0 <= n < n_items and mode[n] == "V":
                 inter(n, "V")

@@ -45,6 +45,7 @@ NARROW = (("v", 0),)
 FIRST_LOADS = ("v", "v")
 X_STEP = -1
 V_WIDENS = 1
+V_ROWS = 2
 LEAD_VW = 2
 W_GROUPS = (("q", 0, 512, "VSVS"), ("q", 512, 512, "VTVS"), ("k", 0, 512, "VTVH"), ("k", 512, 512, "VTVH"), ("q", 1024, 512, "VSVH"), ("q", 1536, 512, "VTVH"), ("k", 1024, 512, "VTVV"), ("k", 1536, 512, "VUVV"))
 V_CHUNKS = ((0, 512, False), (512, 512, True), (1024, 512, True), (1536, 512, False))
@@ -272,7 +273,7 @@ def tile_selfattention_kernel(tc, x, Wq, Wk, Wv_bytes, Wv_scale, st_pos, out_0, 
             wd = wide.tile([P, 4, width], BF16, name="wd")
             lo = col - u[1]
             for j in range(4):
-                if n >= n_items - V_WIDENS:
+                if 4 * (n_items - 1 - n) + (3 - j) < V_ROWS:
                     nc.vector.tensor_scalar(out=wd[:, j, :], in0=units[u][:, j, lo : lo + width].bitcast(FP8), scalar1=vsc[:, g, j : j + 1],
                                             scalar2=None, op0=ALU.mult)
                 else:
@@ -342,10 +343,13 @@ def tile_selfattention_kernel(tc, x, Wq, Wk, Wv_bytes, Wv_scale, st_pos, out_0, 
                 v_pass(t, g, cv, sv)
 
         def v_out(col, width, engs):
-            for t in range(2):
-                ot = outp.tile([P, width], F32, name="ot")
-                evac(engs[t], ot[:], acc[t][:])
-                nc.sync.dma_start(out=out_2[t].rearrange("s h d -> s (h d)")[:, col : col + width], in_=ot[:])
+            pieces = 2 if engs[0] != engs[1] else 1
+            for hf in range(pieces):
+                for t in range(2):
+                    w = width // pieces
+                    ot = outp.tile([P, w], F32, name="ot")
+                    evac(engs[t], ot[:], acc[t][:, w * hf : w * (hf + 1)])
+                    nc.sync.dma_start(out=out_2[t].rearrange("s h d -> s (h d)")[:, col + w * hf : col + w * (hf + 1)], in_=ot[:])
 
         head_queue = []
         multiplied = []

@@ -47,7 +47,7 @@ X_STEP = -1
 V_WIDENS = 1
 V_ROWS = 2
 LEAD_VW = 2
-W_GROUPS = (("q", 0, 512, "VSVS"), ("q", 512, 512, "VTVS"), ("k", 0, 512, "VTVH"), ("k", 512, 512, "VTVH"), ("q", 1024, 512, "VSVH"), ("q", 1536, 512, "VTVH"), ("k", 1024, 512, "VTVV"), ("k", 1536, 512, "VUVV"))
+W_GROUPS = (("q", 0, 512, "VSVS"), ("q", 512, 512, "VTVS"), ("q", 1024, 512, "VTVH"), ("q", 1536, 512, "VTVH"), ("k", 1024, 512, "VSVH"), ("k", 1536, 512, "VTVH"), ("k", 512, 512, "VTVV"), ("k", 0, 512, "VUVV"))
 V_CHUNKS = ((0, 512, False), (512, 512, True), (1024, 512, True), (1536, 512, False))
 PATTERN = "vvvvv" + "wwwwv" * 7 + "wwwwvvvv"
 
@@ -180,10 +180,14 @@ def tile_selfattention_kernel(tc, x, Wq, Wk, Wv_bytes, Wv_scale, st_pos, out_0, 
             load_next(kind)
         nc.sync.dma_start(out=x_sb[:], in_=x.rearrange("b s d -> s b d"))
 
-        pidx = const.tile([P, 1], I32, name="pidx")
-        nc.gpsimd.iota(pidx[:], pattern=[[0, 1]], base=0, channel_multiplier=1)
-        hidx = const.tile([P, HEADS], I32, name="hidx")
-        nc.gpsimd.iota(hidx[:], pattern=[[1, HEADS]], base=0, channel_multiplier=0)
+        pidx = const.tile([P, 7], I32, name="pidx")
+        nc.gpsimd.iota(pidx[:], pattern=[[0, 7]], base=0, channel_multiplier=1)
+        place = const.tile([P, 7], I32, name="place")
+        nc.gpsimd.iota(place[:], pattern=[[1, 7]], base=0, channel_multiplier=0)
+        hidx = const.tile([P, 2, HEADS], I32, name="hidx")
+        nc.gpsimd.iota(hidx[:], pattern=[[0, 2], [1, HEADS]], base=0, channel_multiplier=0)
+        two_e = const.tile([P, 2], I32, name="two_e")
+        nc.gpsimd.iota(two_e[:], pattern=[[-1, 2]], base=2, channel_multiplier=0)
         ident = const.tile([P, P], F32, name="ident")
         make_identity(nc, ident[:])
         ident_b = const.tile([P, P], BF16, name="ident_b")
@@ -194,46 +198,37 @@ def tile_selfattention_kernel(tc, x, Wq, Wk, Wv_bytes, Wv_scale, st_pos, out_0, 
         warm = const.tile([P, 1], F32, name="warm")
         nc.scalar.activation(out=warm[:], in_=zero[:], func=ACT.Sin)
 
-        bits = const.tile([P, 7], I32, name="bits")
+        ratio = const.tile([P, 7], F32, name="ratio")
         for b in range(7):
-            nc.vector.tensor_scalar(out=bits[:, b : b + 1], in0=pidx[:], scalar1=b, scalar2=1,
-                                    op0=ALU.logical_shift_right, op1=ALU.bitwise_and)
+            nc.vector.tensor_scalar(out=ratio[:, b : b + 1], in0=zero[:], scalar1=(ROPE_BASE ** (-(2.0 ** (b - 1)) / 64.0) if b else 0.0),
+                                    scalar2=None, op0=ALU.add)
+        shifted = const.tile([P, 7], I32, name="shifted")
+        nc.vector.tensor_tensor(out=shifted[:], in0=pidx[:], in1=place[:], op=ALU.logical_shift_right)
+        bits = const.tile([P, 7], I32, name="bits")
+        nc.vector.tensor_scalar(out=bits[:], in0=shifted[:], scalar1=1, scalar2=None, op0=ALU.bitwise_and)
         fac = const.tile([P, 7], F32, name="fac")
-        for b in range(1, 7):
-            ratio = ROPE_BASE ** (-(2.0 ** (b - 1)) / 64.0)
-            nc.vector.tensor_scalar(out=fac[:, b : b + 1], in0=bits[:, b : b + 1], scalar1=ratio - 1.0, scalar2=1.0,
-                                    op0=ALU.mult, op1=ALU.add)
-        th3 = const.tile([P, 3], F32, name="th3")
-        nc.vector.tensor_tensor(out=th3[:], in0=fac[:, 1:4], in1=fac[:, 4:7], op=ALU.mult)
-        th1 = const.tile([P, 1], F32, name="th1")
-        nc.vector.tensor_tensor(out=th1[:], in0=th3[:, 0:1], in1=th3[:, 1:2], op=ALU.mult)
+        nc.vector.scalar_tensor_tensor(out=fac[:], in0=bits[:], scalar=0.0, in1=ratio[:], op0=ALU.is_equal, op1=ALU.max)
         theta = const.tile([P, 1], F32, name="theta")
-        nc.vector.tensor_tensor(out=theta[:], in0=th1[:], in1=th3[:, 2:3], op=ALU.mult)
+        nc.vector.tensor_reduce(out=theta[:], in_=fac[:, 1:7], axis=mybir.AxisListType.X, op=ALU.mult)
         phase = const.tile([P, 2], F32, name="phase")
-        nc.vector.tensor_scalar(out=phase[:, 0:1], in0=bits[:, 0:1], scalar1=PI / 2, scalar2=PI / 2, op0=ALU.mult, op1=ALU.add)
-        nc.vector.tensor_scalar(out=phase[:, 1:2], in0=bits[:, 0:1], scalar1=PI / 2, scalar2=None, op0=ALU.mult)
-        ang = const.tile([P, 2 * HEADS], F32, name="ang")
-        for e in range(2):
-            nc.vector.tensor_scalar(out=ang[:, HEADS * e : HEADS * (e + 1)], in0=hidx[:], scalar1=theta[:, 0:1],
-                                    scalar2=phase[:, e : e + 1], op0=ALU.mult, op1=ALU.add)
-        turn1 = const.tile([P, 2 * HEADS], F32, name="turn1")
-        nc.vector.tensor_scalar(out=turn1[:], in0=ang[:], scalar1=PI, scalar2=None, op0=ALU.is_ge)
-        turn2 = const.tile([P, 2 * HEADS], F32, name="turn2")
-        nc.vector.scalar_tensor_tensor(out=turn2[:], in0=ang[:], scalar=3 * PI, in1=turn1[:], op0=ALU.is_ge, op1=ALU.add)
-        turn3 = const.tile([P, 2 * HEADS], F32, name="turn3")
-        nc.vector.scalar_tensor_tensor(out=turn3[:], in0=ang[:], scalar=5 * PI, in1=turn2[:], op0=ALU.is_ge, op1=ALU.add)
-        red = const.tile([P, 2 * HEADS], F32, name="red")
-        nc.vector.scalar_tensor_tensor(out=red[:], in0=turn3[:], scalar=-2 * PI, in1=ang[:], op0=ALU.mult, op1=ALU.add)
-        entry = const.tile([P, 2 * HEADS], F32, name="entry")
+        nc.vector.tensor_scalar(out=phase[:], in0=two_e[:], scalar1=fac[:, 0:1], scalar2=PI / 2, op0=ALU.subtract, op1=ALU.mult)
+        ang = const.tile([P, 2, HEADS], F32, name="ang")
+        nc.vector.scalar_tensor_tensor(out=ang[:], in0=hidx[:], scalar=theta[:, 0:1], in1=phase[:].unsqueeze(2).to_broadcast([P, 2, HEADS]),
+                                       op0=ALU.mult, op1=ALU.add)
+        turns = const.tile([P, 2, HEADS], I32, name="turns")
+        nc.vector.tensor_scalar(out=turns[:], in0=ang[:], scalar1=1.0 / (2 * PI), scalar2=None, op0=ALU.mult)
+        red = const.tile([P, 2, HEADS], F32, name="red")
+        nc.vector.scalar_tensor_tensor(out=red[:], in0=turns[:], scalar=-2 * PI, in1=ang[:], op0=ALU.mult, op1=ALU.add)
+        entry = const.tile([P, 2, HEADS], F32, name="entry")
         nc.scalar.activation(out=entry[:], in_=red[:], func=ACT.Sin)
         pairs = const.tile([P, P // 2], F32, name="pairs")
         id_v = ident[:].rearrange("p (i e) -> p i e", e=2)
         nc.vector.tensor_tensor(out=pairs[:].unsqueeze(2), in0=id_v[:, :, 0:1], in1=id_v[:, :, 1:2], op=ALU.add)
-        rmat = const.tile([P, HEADS, P], F32, name="rmat")
-        full = [P, HEADS, P // 2, 2]
+        rmat = const.tile([P, HEADS - 1, P], F32, name="rmat")
+        full = [P, HEADS - 1, P // 2, 2]
         nc.vector.tensor_tensor(out=rmat[:].rearrange("p h (i e) -> p h i e", e=2),
                                 in0=pairs[:].unsqueeze(1).unsqueeze(3).to_broadcast(full),
-                                in1=entry[:].rearrange("p (e h) -> p h e", e=2).unsqueeze(2).to_broadcast(full), op=ALU.mult)
+                                in1=entry[:].rearrange("p e h -> p h e")[:, 1:HEADS, :].unsqueeze(2).to_broadcast(full), op=ALU.mult)
 
         def evac(eng, dst, src):
             if eng == "S":
@@ -246,7 +241,7 @@ def tile_selfattention_kernel(tc, x, Wq, Wk, Wv_bytes, Wv_scale, st_pos, out_0, 
         words = x_sb[:].rearrange("p b d -> p (b d)").bitcast(F32)
 
         def x_transpose(g):
-            xt = psum.tile([P, 512], F32, name=("tT" if g < 3 else "rot"))
+            xt = psum.tile([P, 512], F32, name="tT", bufs=4)
             for t in range(2):
                 for u in range(2):
                     lo = 1024 * t + 256 * g + u
@@ -357,10 +352,15 @@ def tile_selfattention_kernel(tc, x, Wq, Wk, Wv_bytes, Wv_scale, st_pos, out_0, 
         rotated = []
         slot = [0]
 
+        def first_head(hd):
+            return hd["col"] == 0 and hd["hh"] == 0
+
         def head_matmul(hd):
+            if first_head(hd):
+                return
             cq, sq = code[(hd["mat"], hd["col"])]
             hh = hd["hh"]
-            tt = psum.tile([P, 256], F32, name="tT")
+            tt = psum.tile([P, 256], F32, name="tT", bufs=4)
             for g in range(4):
                 nc.tensor.matmul_mx(out=tt[:], lhsT=cq[:, g, 128 * hh : 128 * (hh + 1)].bitcast(FP8X4),
                                     lhsT_scale=sq[:, g, 128 * hh : 128 * (hh + 1)], rhs=xq[:, g, :].bitcast(FP8X4),
@@ -368,16 +368,26 @@ def tile_selfattention_kernel(tc, x, Wq, Wk, Wv_bytes, Wv_scale, st_pos, out_0, 
             hd["tt"] = tt
 
         def head_evac(hd):
+            if first_head(hd):
+                return
             ts = tsb.tile([P, 256], F32, name="ts")
             evac("S", ts[:], hd["tt"][:])
             hd["ts"] = ts
 
         def head_rotate(hd, pair_tile):
+            if first_head(hd):
+                cq, sq = code[(hd["mat"], hd["col"])]
+                for t in range(2):
+                    for g in range(4):
+                        nc.tensor.matmul_mx(out=pair_tile[:, 256 * t : 256 * t + 128], lhsT=xq[:, g, 128 * t : 128 * (t + 1)].bitcast(FP8X4),
+                                            lhsT_scale=xs[:, g, 128 * t : 128 * (t + 1)], rhs=cq[:, g, 0:128].bitcast(FP8X4),
+                                            rhs_scale=sq[:, g, 0:128], start=(g == 0), stop=(g == 3))
+                return
             ts = hd["ts"]
             hl = hd["hh"] % 2
             for t in range(2):
                 nc.tensor.matmul(out=pair_tile[:, 256 * t + 128 * hl : 256 * t + 128 * (hl + 1)],
-                                 lhsT=ts[:, 128 * t : 128 * (t + 1)], rhs=rmat[:, hd["col"] // 128 + hd["hh"], :], start=True, stop=True)
+                                 lhsT=ts[:, 128 * t : 128 * (t + 1)], rhs=rmat[:, hd["col"] // 128 + hd["hh"] - 1, :], start=True, stop=True)
 
         def pair_out(hd, pair_tile, eng):
             ot = outp.tile([P, 512], F32, name="ot")
@@ -408,7 +418,7 @@ def tile_selfattention_kernel(tc, x, Wq, Wk, Wv_bytes, Wv_scale, st_pos, out_0, 
                 hd = emptied[0][0]
                 emptied.remove(emptied[0])
                 if hd["hh"] % 2 == 0:
-                    pair_now[0] = psum.tile([P, 512], F32, name="rot")
+                    pair_now[0] = psum.tile([P, 512], F32, name="rot", bufs=2)
                 head_rotate(hd, pair_now[0])
                 if hd["hh"] % 2 == 1:
                     rotated.append((hd, pair_now[0], slot[0]))

import math
from contextlib import ExitStack

import concourse.mybir as mybir
from concourse.masks import make_identity

F32 = mybir.dt.float32
BF16 = mybir.dt.bfloat16
U32 = mybir.dt.uint32
U8 = mybir.dt.uint8
I32 = mybir.dt.int32
FP8 = mybir.dt.float8_e4m3fn
FP8X4 = mybir.dt.float8_e4m3fn_x4
ALU = mybir.AluOpType
ACT = mybir.ActivationFunctionType

FLOPS = 2 * 256 * 2048 * 6144

P = 128
HEADS = 16
ROPE_BASE = 10000.0
PI = 3.141592653589793

N_RAW = 8
N_BYT = 6
N_WIDE = 7
N_GRP = 7
N_COD = 3
N_CODV = 6
N_TSB = 6
N_OUT = 8
LEAD_WIDEN = 5
LOAD_LEAD = 10
LEAD_SINT = 3
LEAD_T = 6
LAG_T = 2
LAG_O = 3
LAG_R = 1
LAG_V = 2
LAG_B = 3
X_ENG = "V"
RUN = 2
FAST_END = 8
NARROW = (("v", 0),)
FIRST_LOADS = ("v", "v")
X_STEP = -1
V_WIDENS = 1
V_ROWS = 2
LEAD_VW = 2
W_GROUPS = (("q", 0, 512, "VSVS"), ("q", 512, 512, "VTVS"), ("q", 1024, 512, "VTVH"), ("q", 1536, 512, "VTVH"), ("k", 1024, 512, "VSVH"), ("k", 1536, 512, "VTVH"), ("k", 512, 512, "VTVV"), ("k", 0, 512, "VUVV"))
V_CHUNKS = ((0, 512, False), (512, 512, True), (1024, 512, True), (1536, 512, False))
PATTERN = "vvvvv" + "wwwwv" * 7 + "wwwwvvvv"


def build_order():
    v_items = [("v", col, width, g) for (col, width, at_once) in V_CHUNKS for g in range(4)]
    w_items = [(mat, col, width, g) for (mat, col, width, plan) in W_GROUPS for g in range(4)]
    order = []
    for ch in PATTERN:
        if ch == "v":
            order.append(v_items[0])
            v_items = v_items[1:]
        else:
            order.append(w_items[0])
            w_items = w_items[1:]
    assert not v_items and not w_items
    return order


def tile_selfattention_kernel(tc, x, Wq, Wk, Wv_bytes, Wv_scale, st_pos, out_0, out_1, out_2):
    nc = tc.nc
    order = build_order()
    n_items = len(order)
    weights = {"q": Wq, "k": Wk}
    outs = {"q": out_0, "k": out_1, "v": out_2}

    with ExitStack() as ctx:
        const = ctx.enter_context(tc.tile_pool(name="const", bufs=1))
        raw = ctx.enter_context(tc.tile_pool(name="raw", bufs=N_RAW))
        byt = ctx.enter_context(tc.tile_pool(name="byt", bufs=N_BYT))
        wide = ctx.enter_context(tc.tile_pool(name="wide", bufs=N_WIDE))
        grp = ctx.enter_context(tc.tile_pool(name="grp", bufs=N_GRP))
        cod = ctx.enter_context(tc.tile_pool(name="cod", bufs=N_COD))
        codv = ctx.enter_context(tc.tile_pool(name="codv", bufs=N_CODV))
        tsb = ctx.enter_context(tc.tile_pool(name="tsb", bufs=N_TSB))
        outp = ctx.enter_context(tc.tile_pool(name="outp", bufs=N_OUT))
        psum = ctx.enter_context(tc.psum_pool(name="psum", bufs=3))
        ctx.enter_context(tc.manual_schedule())

        plans = {}
        for (mat, col, width, plan) in W_GROUPS:
            plans[(mat, col)] = plan
        at_once = {}
        for (col, width, flag) in V_CHUNKS:
            at_once[col] = flag
        mode = {}
        for n, it in enumerate(order):
            mode[n] = "V" if it[0] == "v" else plans[(it[0], it[1])][it[3]]
            assert mode[n] in ("V", "S") or it[2] == 512

        tpos = {}
        for n, it in enumerate(order):
            tpos[n] = sum([o[2] for o in order[:n]]) / 512.0

        def step_for(n, lead):
            target = tpos[n] - lead
            if target < 0:
                return int(math.floor(target))
            return max([m for m in range(n_items) if tpos[m] <= target])

        widen_at = {}
        pe_at = {}
        s_at = {}
        for n, it in enumerate(order):
            if it[0] == "v":
                widen_at.setdefault(step_for(n, LEAD_VW if n >= n_items - V_WIDENS else LEAD_WIDEN), []).append(n)
            if mode[n] in ("T", "U"):
                pe_at.setdefault(step_for(n, LEAD_T), []).append(n)
            if mode[n] in ("S", "T", "H", "U"):
                s_at.setdefault(step_for(n, LEAD_SINT), []).append(n)

        def unit_of(it):
            mat, col, width, g = it
            if (mat, col // 1024) in NARROW:
                return (mat, 512 * (col // 512), 512, g)
            return (mat, 1024 * (col // 1024), 1024, g)

        need = {}
        for n, it in enumerate(order):
            if unit_of(it) not in need:
                need[unit_of(it)] = step_for(n, LEAD_WIDEN if it[0] == "v" else (LEAD_T if mode[n] in ("T", "U") else LEAD_SINT))
        load_list = sorted(need, key=lambda u: need[u])
        room = {"v": N_BYT, "w": N_RAW}
        pending = {"v": [u for u in load_list if u[0] == "v"], "w": [u for u in load_list if u[0] != "v"]}
        live = {"v": [], "w": []}
        units = {}
        reads_left = {}

        def load(u):
            mat, col, width, g = u
            rows = slice(512 * g, 512 * (g + 1))
            cols = slice(col, col + width)
            if mat == "v":
                t = byt.tile([P, 4, width], U8, name="vb")
                src = Wv_bytes
            else:
                t = raw.tile([P, 4, width], BF16, name="rw", align_bytes=64)
                src = weights[mat]
            nc.sync.dma_start(out=t[:], in_=src[rows, cols].rearrange("(p j) n -> p j n", j=4))
            units[u] = t
            reads_left[u] = len([it for it in order if unit_of(it) == u])
            live["v" if mat == "v" else "w"].append(u)

        def load_next(kind):
            nxt = pending[kind][0]
            pending[kind].remove(nxt)
            load(nxt)

        def unit_read(u):
            reads_left[u] = reads_left[u] - 1

        def issue_loads(step):
            for u in load_list:
                kind = "v" if u[0] == "v" else "w"
                if u in pending[kind] and need[u] - LOAD_LEAD <= step and pending[kind][0] == u:
                    if len(live[kind]) == room[kind]:
                        if reads_left[live[kind][0]] > 0:
                            continue
                        live[kind].remove(live[kind][0])
                    load_next(kind)

        vsc = const.tile([P, 4, 4], F32, name="vsc")
        nc.scalar.dma_start(out=vsc[:], in_=Wv_scale.rearrange("(g p j) o -> p g (j o)", p=P, j=4))
        x_sb = raw.tile([P, 2, 2048], BF16, name="rw", align_bytes=64)
        xg = raw.tile([P, 4, 1024], BF16, name="rw", align_bytes=64)
        for u in (("x", 0, 0, 0), ("x", 1, 0, 0)):
            live["w"].append(u)
            reads_left[u] = 1
        for kind in FIRST_LOADS:
            load_next(kind)
        nc.sync.dma_start(out=x_sb[:], in_=x.rearrange("b s d -> s b d"))

        pidx = const.tile([P, 7], I32, name="pidx")
        nc.gpsimd.iota(pidx[:], pattern=[[0, 7]], base=0, channel_multiplier=1)
        place = const.tile([P, 7], I32, name="place")
        nc.gpsimd.iota(place[:], pattern=[[1, 7]], base=0, channel_multiplier=0)
        hidx = const.tile([P, 2, HEADS], I32, name="hidx")
        nc.gpsimd.iota(hidx[:], pattern=[[0, 2], [1, HEADS]], base=0, channel_multiplier=0)
        two_e = const.tile([P, 2], I32, name="two_e")
        nc.gpsimd.iota(two_e[:], pattern=[[-1, 2]], base=2, channel_multiplier=0)
        ident = const.tile([P, P], F32, name="ident")
        make_identity(nc, ident[:])
        ident_b = const.tile([P, P], BF16, name="ident_b")
        make_identity(nc, ident_b[:])

        zero = const.tile([P, 1], F32, name="zero")
        nc.vector.memset(zero[:], 0.0)
        warm = const.tile([P, 1], F32, name="warm")
        nc.scalar.activation(out=warm[:], in_=zero[:], func=ACT.Sin)

        ratio = const.tile([P, 7], F32, name="ratio")
        for b in range(7):
            nc.vector.tensor_scalar(out=ratio[:, b : b + 1], in0=zero[:], scalar1=(ROPE_BASE ** (-(2.0 ** (b - 1)) / 64.0) if b else 0.0),
                                    scalar2=None, op0=ALU.add)
        shifted = const.tile([P, 7], I32, name="shifted")
        nc.vector.tensor_tensor(out=shifted[:], in0=pidx[:], in1=place[:], op=ALU.logical_shift_right)
        bits = const.tile([P, 7], I32, name="bits")
        nc.vector.tensor_scalar(out=bits[:], in0=shifted[:], scalar1=1, scalar2=None, op0=ALU.bitwise_and)
        fac = const.tile([P, 7], F32, name="fac")
        nc.vector.scalar_tensor_tensor(out=fac[:], in0=bits[:], scalar=0.0, in1=ratio[:], op0=ALU.is_equal, op1=ALU.max)
        theta = const.tile([P, 1], F32, name="theta")
        nc.vector.tensor_reduce(out=theta[:], in_=fac[:, 1:7], axis=mybir.AxisListType.X, op=ALU.mult)
        phase = const.tile([P, 2], F32, name="phase")
        nc.vector.tensor_scalar(out=phase[:], in0=two_e[:], scalar1=fac[:, 0:1], scalar2=PI / 2, op0=ALU.subtract, op1=ALU.mult)
        ang = const.tile([P, 2, HEADS], F32, name="ang")
        nc.vector.scalar_tensor_tensor(out=ang[:], in0=hidx[:], scalar=theta[:, 0:1], in1=phase[:].unsqueeze(2).to_broadcast([P, 2, HEADS]),
                                       op0=ALU.mult, op1=ALU.add)
        turns = const.tile([P, 2, HEADS], I32, name="turns")
        nc.vector.tensor_scalar(out=turns[:], in0=ang[:], scalar1=1.0 / (2 * PI), scalar2=None, op0=ALU.mult)
        red = const.tile([P, 2, HEADS], F32, name="red")
        nc.vector.scalar_tensor_tensor(out=red[:], in0=turns[:], scalar=-2 * PI, in1=ang[:], op0=ALU.mult, op1=ALU.add)
        entry = const.tile([P, 2, HEADS], F32, name="entry")
        nc.scalar.activation(out=entry[:], in_=red[:], func=ACT.Sin)
        pairs = const.tile([P, P // 2], F32, name="pairs")
        id_v = ident[:].rearrange("p (i e) -> p i e", e=2)
        nc.vector.tensor_tensor(out=pairs[:].unsqueeze(2), in0=id_v[:, :, 0:1], in1=id_v[:, :, 1:2], op=ALU.add)
        rmat = const.tile([P, HEADS - 1, P], F32, name="rmat")
        full = [P, HEADS - 1, P // 2, 2]
        nc.vector.tensor_tensor(out=rmat[:].rearrange("p h (i e) -> p h i e", e=2),
                                in0=pairs[:].unsqueeze(1).unsqueeze(3).to_broadcast(full),
                                in1=entry[:].rearrange("p e h -> p h e")[:, 1:HEADS, :].unsqueeze(2).to_broadcast(full), op=ALU.mult)

        def evac(eng, dst, src):
            if eng == "S":
                nc.scalar.copy(out=dst, in_=src)
            else:
                nc.vector.tensor_copy(out=dst, in_=src)

        xq = const.tile([P, 4, 256], U32, name="xq", align_bytes=64)
        xs = const.tile([P, 4, 256], U8, name="xs", align_bytes=64)
        words = x_sb[:].rearrange("p b d -> p (b d)").bitcast(F32)

        def x_transpose(g):
            xt = psum.tile([P, 512], F32, name="tT", bufs=4)
            for t in range(2):
                for u in range(2):
                    lo = 1024 * t + 256 * g + u
                    nc.tensor.transpose(xt[:, 128 * (2 * t + u) : 128 * (2 * t + u + 1)], words[:, lo : lo + 255 : 2], ident[:])
            evac(X_ENG, xg[:, g, :].bitcast(F32).rearrange("p (t r u) -> p t r u", t=2, u=2),
                 xt[:].rearrange("p (t u r) -> p t r u", t=2, u=2))

        def x_quant():
            nc.vector.quantize_mx(out=xq[:].rearrange("p g n -> p (g n)").bitcast(FP8X4), scales=xs[:].rearrange("p g n -> p (g n)"),
                                  in_=xg[:].rearrange("p g n -> p (g n)"))

        wd_tiles = {}
        gr_tiles = {}
        code = {}
        acc = {}
        tasks = {}

        def later(step, fn):
            tasks.setdefault(step, []).append(fn)

        def widen(n):
            mat, col, width, g = order[n]
            u = unit_of(order[n])
            wd = wide.tile([P, 4, width], BF16, name="wd")
            lo = col - u[1]
            for j in range(4):
                if 4 * (n_items - 1 - n) + (3 - j) < V_ROWS:
                    nc.vector.tensor_scalar(out=wd[:, j, :], in0=units[u][:, j, lo : lo + width].bitcast(FP8), scalar1=vsc[:, g, j : j + 1],
                                            scalar2=None, op0=ALU.mult)
                else:
                    nc.scalar.activation(out=wd[:, j, :], in_=units[u][:, j, lo : lo + width].bitcast(FP8), func=ACT.Copy,
                                         scale=vsc[:, g, j : j + 1])
            wd_tiles[n] = wd
            unit_read(u)

        def inter(n, eng, part=None):
            mat, col, width, g = order[n]
            if part != 1:
                gr_new = grp.tile([P, 4 * width], BF16, name="gr", align_bytes=64)
                gr_tiles[n] = gr_new
            gr = gr_tiles[n]
            if mat == "v":
                src = wd_tiles[n][:]
            else:
                lo = col - unit_of(order[n])[1]
                src = units[unit_of(order[n])][:, :, lo : lo + width]
            dst = gr[:]
            if part is not None:
                src = src[:, :, (width // 2) * part : (width // 2) * (part + 1)]
                dst = gr[:, 2 * width * part : 2 * width * (part + 1)]
            evac(eng, dst.rearrange("p (c i j) -> p c j i", i=RUN, j=4), src.rearrange("p j (c i) -> p c j i", i=RUN))
            if mat != "v" and part != 0:
                unit_read(unit_of(order[n]))

        il_tiles = {}

        def pe_inter(n):
            mat, col, width, g = order[n]
            u = unit_of(order[n])
            for hf in range(1 if mode[n] == "U" else 2):
                il = psum.tile([P, 1024], BF16, name="aux", bufs=2)
                for q in range(2):
                    lo = col - u[1] + 256 * hf + 128 * q
                    nc.tensor.matmul(out=il[:, 512 * q : 512 * (q + 1)].rearrange("p (c j) -> p c j", j=4), lhsT=ident_b[:],
                                     rhs=units[u][:, :, lo : lo + 128].rearrange("p j c -> p c j"), start=True, stop=True)
                il_tiles[(n, hf)] = il
            if mode[n] == "T":
                unit_read(u)

        def pe_inter_out(n):
            gr = grp.tile([P, 2048], BF16, name="gr", align_bytes=64)
            for hf in range(1 if mode[n] == "U" else 2):
                nc.scalar.copy(out=gr[:, 1024 * hf : 1024 * (hf + 1)], in_=il_tiles[(n, hf)][:])
            gr_tiles[n] = gr

        v_codes = {}

        def v_pass(t, g, cv, sv):
            nc.tensor.matmul_mx(out=acc[t][:], lhsT=xq[:, g, 128 * t : 128 * (t + 1)].bitcast(FP8X4),
                                lhsT_scale=xs[:, g, 128 * t : 128 * (t + 1)], rhs=cv[:].bitcast(FP8X4), rhs_scale=sv[:],
                                start=(g == 0), stop=(g == 3))

        def v_burst(col, width):
            for t in range(2):
                acc[t] = psum.tile([P, width], F32, name="aux", bufs=2)
                for g in range(4):
                    v_pass(t, g, v_codes[(col, g)][0], v_codes[(col, g)][1])

        def v_matmul(n, cv, sv):
            mat, col, width, g = order[n]
            for t in range(2):
                if g == 0:
                    acc[t] = psum.tile([P, width], F32, name="aux", bufs=2)
                v_pass(t, g, cv, sv)

        def v_out(col, width, engs):
            pieces = 2 if engs[0] != engs[1] else 1
            for hf in range(pieces):
                for t in range(2):
                    w = width // pieces
                    ot = outp.tile([P, w], F32, name="ot")
                    evac(engs[t], ot[:], acc[t][:, w * hf : w * (hf + 1)])
                    nc.sync.dma_start(out=out_2[t].rearrange("s h d -> s (h d)")[:, col + w * hf : col + w * (hf + 1)], in_=ot[:])

        head_queue = []
        multiplied = []
        emptied = []
        rotated = []
        slot = [0]

        def first_head(hd):
            return hd["col"] == 0 and hd["hh"] == 0

        def head_matmul(hd):
            if first_head(hd):
                return
            cq, sq = code[(hd["mat"], hd["col"])]
            hh = hd["hh"]
            tt = psum.tile([P, 256], F32, name="tT", bufs=4)
            for g in range(4):
                nc.tensor.matmul_mx(out=tt[:], lhsT=cq[:, g, 128 * hh : 128 * (hh + 1)].bitcast(FP8X4),
                                    lhsT_scale=sq[:, g, 128 * hh : 128 * (hh + 1)], rhs=xq[:, g, :].bitcast(FP8X4),
                                    rhs_scale=xs[:, g, :], start=(g == 0), stop=(g == 3))
            hd["tt"] = tt

        def head_evac(hd):
            if first_head(hd):
                return
            ts = tsb.tile([P, 256], F32, name="ts")
            evac("S", ts[:], hd["tt"][:])
            hd["ts"] = ts

        def head_rotate(hd, pair_tile):
            if first_head(hd):
                cq, sq = code[(hd["mat"], hd["col"])]
                for t in range(2):
                    for g in range(4):
                        nc.tensor.matmul_mx(out=pair_tile[:, 256 * t : 256 * t + 128], lhsT=xq[:, g, 128 * t : 128 * (t + 1)].bitcast(FP8X4),
                                            lhsT_scale=xs[:, g, 128 * t : 128 * (t + 1)], rhs=cq[:, g, 0:128].bitcast(FP8X4),
                                            rhs_scale=sq[:, g, 0:128], start=(g == 0), stop=(g == 3))
                return
            ts = hd["ts"]
            hl = hd["hh"] % 2
            for t in range(2):
                nc.tensor.matmul(out=pair_tile[:, 256 * t + 128 * hl : 256 * t + 128 * (hl + 1)],
                                 lhsT=ts[:, 128 * t : 128 * (t + 1)], rhs=rmat[:, hd["col"] // 128 + hd["hh"] - 1, :], start=True, stop=True)

        def pair_out(hd, pair_tile, eng):
            ot = outp.tile([P, 512], F32, name="ot")
            evac(eng, ot[:], pair_tile[:])
            lo = hd["col"] + 128 * (hd["hh"] - 1)
            nc.sync.dma_start(out=outs[hd["mat"]].rearrange("b s h d -> s b (h d)")[:, :, lo : lo + 256],
                              in_=ot[:].rearrange("p (t n) -> p t n", t=2))

        pair_now = [None]

        def epilogue_slot(drain):
            slot[0] += 1
            if rotated and (rotated[0][2] + LAG_O <= slot[0] or (drain and not head_queue and not multiplied and not emptied)):
                hd, pt, born = rotated[0]
                rotated.remove(rotated[0])
                pair_out(hd, pt, "S")
            if head_queue:
                hd = head_queue[0]
                head_queue.remove(hd)
                head_matmul(hd)
                multiplied.append((hd, slot[0]))
            if multiplied and (multiplied[0][1] + LAG_T <= slot[0] or (drain and not head_queue)):
                hd = multiplied[0][0]
                multiplied.remove(multiplied[0])
                head_evac(hd)
                emptied.append((hd, slot[0]))
            if emptied and (emptied[0][1] + LAG_R <= slot[0] or (drain and not head_queue and not multiplied)):
                hd = emptied[0][0]
                emptied.remove(emptied[0])
                if hd["hh"] % 2 == 0:
                    pair_now[0] = psum.tile([P, 512], F32, name="rot", bufs=2)
                head_rotate(hd, pair_now[0])
                if hd["hh"] % 2 == 1:
                    rotated.append((hd, pair_now[0], slot[0]))

        def quant(n, step):
            mat, col, width, g = order[n]
            if mat == "v":
                cv = codv.tile([P, width], U32, name="cv", align_bytes=64)
                sv = codv.tile([P, width], U8, name="sv", align_bytes=64)
                nc.vector.quantize_mx(out=cv[:].bitcast(FP8X4), scales=sv[:], in_=gr_tiles[n][:])
                if at_once[col]:
                    v_codes[(col, g)] = (cv, sv)
                    if g == 3:
                        later(step + 1, lambda: v_burst(col, width))
                else:
                    later(step + 1, lambda: v_matmul(n, cv, sv))
                if g == 3:
                    last = n == n_items - 1
                    later(step + (1 if last else (LAG_B if at_once[col] else LAG_V)),
                          lambda: v_out(col, width, ("S", "V") if last else ("S", "S")))
                return
            if g == 0:
                cq_new = cod.tile([P, 4, width], U32, name="cq", align_bytes=64)
                sq_new = cod.tile([P, 4, width], U8, name="sq", align_bytes=64)
                code[(mat, col)] = (cq_new, sq_new)
            cq, sq = code[(mat, col)]
            nc.vector.quantize_mx(out=cq[:, g, :].bitcast(FP8X4), scales=sq[:, g, :], in_=gr_tiles[n][:])
            if g == 3:
                for hh in range(width // 128):
                    head_queue.append({"mat": mat, "col": col, "hh": hh})

        credit = [0.0]
        step = -LEAD_WIDEN - 1
        while step < n_items + 2 or head_queue or multiplied or emptied or rotated:
            issue_loads(step)
            share = order[step][2] / 512.0 if 0 <= step < n_items else 1.0
            fast = step >= n_items or (step >= 0 and tpos[step] >= tpos[n_items - 1] + order[n_items - 1][2] / 512.0 - FAST_END)
            credit[0] += share * (2 if fast else 1)
            while credit[0] >= 1:
                credit[0] -= 1
                epilogue_slot(step >= n_items)
            for fn in tasks.get(step, []):
                fn()
            for n in widen_at.get(step, []):
                widen(n)
            for n in pe_at.get(step, []):
                pe_inter(n)
            for n in s_at.get(step, []):
                if mode[n] == "S":
                    inter(n, "S")
                elif mode[n] == "H":
                    inter(n, "S", 0)
                else:
                    pe_inter_out(n)
            n = step + 1
            if 0 <= n < n_items and mode[n] in ("H", "U"):
                inter(n, "V", 1)
            if 0 <= n < n_items and mode[n] == "V":
                inter(n, "V")
            if step == X_STEP:
                for g in range(4):
                    x_transpose(g)
                unit_read(("x", 0, 0, 0))
            if 0 <= step < n_items:
                quant(step, step)
            if step == X_STEP + 1:
                x_quant()
                unit_read(("x", 1, 0, 0))
            step += 1
